import numpy as np
import ml_dtypes


def mxq(x, axis, fmt="e4m3"):
    dtype, down = {"e4m3": (ml_dtypes.float8_e4m3fn, 7), "e5m2": (ml_dtypes.float8_e5m2, 14)}[fmt]
    v = np.moveaxis(np.asarray(x, np.float32).astype(ml_dtypes.bfloat16).astype(np.float64), axis, -1)
    blocks = v.reshape(v.shape[:-1] + (-1, 32))
    amax = np.abs(blocks).max(-1, keepdims=True)
    byte = np.maximum(np.where(amax > 0, np.frexp(amax)[1] - 1 + 127, 0) - down, 1)
    scale = np.exp2(byte - 127.0)
    codes = (blocks / scale).astype(np.float32).astype(dtype).astype(np.float64)
    return np.moveaxis((codes * scale).reshape(v.shape), -1, axis)


WIDE = False


def mx_kscale(k):
    if not WIDE:
        return np.ones(k)
    levels = np.array([10, -10, 5, -5, 0])
    a = np.random.permutation(np.resize(levels, k // 512 * 4)).reshape(k // 512, 4)
    idx = np.arange(k)
    return np.exp2(a[idx // 512, idx % 128 // 32])


BF16 = ml_dtypes.bfloat16


def bf(x):
    return np.asarray(x, np.float32).astype(BF16)


def f64(x):
    return np.asarray(x).astype(np.float64)


B, S, DIM, H, NOPE, ROPE, VHD, KV_RANK = 4, 2048, 512, 2, 128, 64, 128, 512
QKHD = NOPE + ROPE
HALF = ROPE // 2
EPS = 1e-5


def rope(u, cos, sin):
    ur = u.reshape(u.shape[:-1] + (HALF, 2))
    a, b = ur[..., 0], ur[..., 1]
    c = cos[None, :, None, :]
    s = sin[None, :, None, :]
    return np.stack([a * c - b * s, a * s + b * c], axis=-1).reshape(u.shape)


def setup_inputs():
    s = mx_kscale(DIM)
    t = mx_kscale(KV_RANK)
    inv_freq = 1.0 / 10000.0 ** (np.arange(0, ROPE, 2) / ROPE)
    ang = np.arange(S)[:, None] * inv_freq[None, :]
    return {"x": bf(np.random.standard_normal((B, S, DIM)) * s),
            "wkv_a_w": bf(np.random.standard_normal((DIM, KV_RANK + H * ROPE)) / np.sqrt(DIM) / s[:, None]),
            "wkv_a_b": bf(np.random.standard_normal(KV_RANK + H * ROPE) * 0.2),
            "kvn_g": bf((1.0 + 0.1 * np.random.standard_normal(KV_RANK)) * t),
            "kvn_b": bf(0.1 * np.random.standard_normal(KV_RANK) * t),
            "wk_w": bf(np.random.standard_normal((KV_RANK, H * NOPE)) / np.sqrt(KV_RANK) / t[:, None]),
            "wk_b": bf(np.random.standard_normal(H * NOPE) * 0.2),
            "wv_w": bf(np.random.standard_normal((KV_RANK, H * VHD)) / np.sqrt(KV_RANK) / t[:, None]),
            "wv_b": bf(np.random.standard_normal(H * VHD) * 0.2),
            "cos": bf(np.cos(ang)), "sin": bf(np.sin(ang))}


def reference(x, wkv_a_w, wkv_a_b, kvn_g, kvn_b, wk_w, wk_b, wv_w, wv_b, cos, sin):
    kv = (mxq(f64(x), 2, "e4m3") @ mxq(f64(wkv_a_w), 0, "e4m3")) + f64(wkv_a_b)
    k_rope = kv[..., : H * ROPE]
    c = kv[..., H * ROPE:]
    mu = c.mean(-1, keepdims=True)
    var = np.square(c - mu).mean(-1, keepdims=True)
    c = (c - mu) / np.sqrt(var + EPS) * f64(kvn_g) + f64(kvn_b)
    cq = mxq(c, 2, "e4m3")
    k_nope = (cq @ mxq(f64(wk_w), 0, "e4m3")) + f64(wk_b)
    v = (cq @ mxq(f64(wv_w), 0, "e4m3")) + f64(wv_b)
    k = np.concatenate([k_nope, k_rope], axis=-1).reshape(B, S, H, QKHD)
    k = np.concatenate([k[..., :NOPE], rope(k[..., NOPE:], f64(cos), f64(sin))], axis=-1)
    return k, v.reshape(B, S, H, VHD)

@@ -1,0 +1,296 @@
+from contextlib import ExitStack
+
+import concourse.mybir as mybir
+from concourse.masks import make_identity
+
+F32 = mybir.dt.float32
+BF16 = mybir.dt.bfloat16
+U32 = mybir.dt.uint32
+U8 = mybir.dt.uint8
+FP8X4 = mybir.dt.float8_e4m3fn_x4
+ALU = mybir.AluOpType
+ACT = mybir.ActivationFunctionType
+
+P = 128
+PACK = 4
+TOKENS = 4 * 2048
+SEQ = 2048
+DIM = 512
+RANK = 512
+ROPE_COLS = 128
+KV_COLS = ROPE_COLS + RANK
+NOPE_COLS = 256
+V_COLS = 256
+K_COLS = NOPE_COLS + ROPE_COLS
+HEADS = 2
+HEAD = K_COLS // HEADS
+ROT = 64
+TILES = 4
+GROUP = TILES * P
+GROUPS = TOKENS // GROUP
+SEQ_GROUPS = SEQ // GROUP
+EPS = 1e-5
+
+FLOPS = 2 * TOKENS * (DIM * KV_COLS + RANK * (NOPE_COLS + V_COLS))
+
+
+def regroup(nc, grouped, planes):
+    nc.vector.tensor_copy(
+        out=grouped.rearrange("p (c i) t -> p c t i", i=4),
+        in_=planes.rearrange("p t (c i) -> p c t i", i=4),
+    )
+
+
+def quantise(nc, codes, scales, grouped):
+    nc.vector.quantize_mx(
+        out=codes.bitcast(FP8X4),
+        scales=scales,
+        in_=grouped.rearrange("p c t -> p (c t)"),
+    )
+
+
+def tile_mla_pa_t_kernel(
+    tc, x, wkv_a_w, wkv_a_b, kvn_g, kvn_b, wk_w, wk_b, wv_w, wv_b, cos, sin, out_0, out_1
+):
+    nc = tc.nc
+    x_rows = x.rearrange("b s d -> (b s) d")
+    k_rows = out_0.rearrange("b s h e -> (b s) (h e)")
+    v_rows = out_1.rearrange("b s h e -> (b s) (h e)")
+
+    with ExitStack() as ctx:
+        consts = ctx.enter_context(tc.tile_pool(name="consts", bufs=1))
+        xin = ctx.enter_context(tc.tile_pool(name="xin", bufs=3))
+        work = ctx.enter_context(tc.tile_pool(name="work", bufs=2))
+        small = ctx.enter_context(tc.tile_pool(name="small", bufs=3))
+        outs = ctx.enter_context(tc.tile_pool(name="outs", bufs=3))
+        psum1 = ctx.enter_context(tc.psum_pool(name="psum1", bufs=1))
+        psum2 = ctx.enter_context(tc.psum_pool(name="psum2", bufs=2))
+
+        def load_x(g):
+            x_sb = xin.tile([P, TILES, DIM], BF16)
+            nc.sync.dma_start(
+                out=x_sb[:],
+                in_=x_rows[g * GROUP : (g + 1) * GROUP, :].rearrange("(p i) d -> p i d", i=TILES),
+            )
+            return x_sb
+
+        x_first = load_x(0)
+
+        w1_raw = consts.tile([P, 2, 2, KV_COLS], BF16)
+        nc.sync.dma_start(out=w1_raw[:], in_=wkv_a_w.rearrange("(u q e) c -> q u e c", u=2, e=2))
+        w2_raw = consts.tile([P, PACK, NOPE_COLS + V_COLS], BF16)
+        nc.sync.dma_start(out=w2_raw[:, :, 0:NOPE_COLS], in_=wk_w.rearrange("(t p) n -> p t n", p=P))
+        nc.sync.dma_start(out=w2_raw[:, :, NOPE_COLS:], in_=wv_w.rearrange("(t p) n -> p t n", p=P))
+
+        b1_bc = consts.tile([P, KV_COLS], BF16)
+        nc.scalar.dma_start(out=b1_bc[:], in_=wkv_a_b.partition_broadcast(P))
+        b2_bc = consts.tile([P, 2, NOPE_COLS], BF16)
+        nc.scalar.dma_start(out=b2_bc[:, 0, :], in_=wk_b.partition_broadcast(P))
+        nc.scalar.dma_start(out=b2_bc[:, 1, :], in_=wv_b.partition_broadcast(P))
+
+        gb_rows = consts.tile([P, P], BF16)
+        nc.vector.memset(gb_rows[:], 0.0)
+        nc.scalar.dma_start(out=gb_rows[0:PACK, :], in_=kvn_g.rearrange("(t p) -> t p", p=P))
+        nc.scalar.dma_start(out=gb_rows[PACK : 2 * PACK, :], in_=kvn_b.rearrange("(t p) -> t p", p=P))
+
+        cos_sb = consts.tile([P, SEQ_GROUPS, TILES, ROT // 2], BF16)
+        nc.scalar.dma_start(out=cos_sb[:], in_=cos.rearrange("(s p i) j -> p s i j", p=P, i=TILES))
+        sin_sb = consts.tile([P, SEQ_GROUPS, TILES, ROT // 2], BF16)
+        nc.scalar.dma_start(out=sin_sb[:], in_=sin.rearrange("(s p i) j -> p s i j", p=P, i=TILES))
+        neg_sin_sb = consts.tile([P, SEQ_GROUPS, TILES, ROT // 2], BF16)
+        nc.vector.tensor_scalar_mul(out=neg_sin_sb[:], in0=sin_sb[:], scalar1=-1.0)
+
+        eps_col = consts.tile([P, 1], F32)
+        nc.vector.memset(eps_col[:], EPS)
+        warm = consts.tile([P, 1], F32)
+        nc.scalar.activation(out=warm[:], in_=eps_col[:], func=ACT.Sqrt)
+
+        ident = consts.tile([P, P], F32)
+        make_identity(nc, ident[:])
+
+        w1_grouped = consts.tile([P, KV_COLS, PACK], BF16, align_bytes=64)
+        w1_codes = consts.tile([P, KV_COLS], U32, align_bytes=64)
+        w1_scales = consts.tile([P, KV_COLS], U8, align_bytes=64)
+        regroup(nc, w1_grouped[:], w1_raw[:].rearrange("p u e c -> p (u e) c"))
+        for cols in (slice(0, ROPE_COLS), slice(ROPE_COLS, KV_COLS)):
+            quantise(nc, w1_codes[:, cols], w1_scales[:, cols], w1_grouped[:, cols, :])
+
+        w2_grouped = consts.tile([P, NOPE_COLS + V_COLS, PACK], BF16, align_bytes=64)
+        w2_codes = consts.tile([P, NOPE_COLS + V_COLS], U32, align_bytes=64)
+        w2_scales = consts.tile([P, NOPE_COLS + V_COLS], U8, align_bytes=64)
+        regroup(nc, w2_grouped[:], w2_raw[:])
+        quantise(nc, w2_codes[:], w2_scales[:], w2_grouped[:])
+
+        gb_f32 = consts.tile([P, P], F32)
+        nc.vector.tensor_copy(out=gb_f32[:], in_=gb_rows[:])
+        gb_t = psum2.tile([P, TILES, P], F32, tag="z_t")
+        nc.tensor.transpose(gb_t[:, 0, :], gb_f32[:], ident[:])
+        gb_col = consts.tile([P, 2 * PACK], F32)
+        nc.vector.tensor_copy(out=gb_col[:], in_=gb_t[:, 0, 0 : 2 * PACK])
+
+        def front(g, x_sb):
+            x_grouped = work.tile([P, GROUP * PACK], BF16, align_bytes=64)
+            x_grouped_words = x_grouped[:].bitcast(F32)
+            for half in range(2):
+                x_t = psum1.tile([P, 2, 2, P], F32)
+                for i in range(2):
+                    x_words = x_sb[:, 2 * half + i, :].bitcast(F32)
+                    for u in range(2):
+                        nc.tensor.transpose(x_t[:, i, u, :], x_words[:, u * P : (u + 1) * P], ident[:])
+                nc.scalar.copy(
+                    out=x_grouped_words[:, half * GROUP : (half + 1) * GROUP].rearrange(
+                        "p (i w u) -> p i w u", i=2, u=2
+                    ),
+                    in_=x_t[:].rearrange("p i u w -> p i w u"),
+                )
+            x_codes = work.tile([P, GROUP], U32, align_bytes=64)
+            x_scales = work.tile([P, GROUP], U8, align_bytes=64)
+            nc.vector.quantize_mx(out=x_codes[:].bitcast(FP8X4), scales=x_scales[:], in_=x_grouped[:])
+
+            kv_out = outs.tile([P, TILES, 2, K_COLS], F32)
+            c = work.tile([P, TILES, RANK], F32)
+            sums = small.tile([P, TILES], F32)
+            k_rope = psum1.tile([P, TILES, ROPE_COLS], F32)
+            for i in range(TILES):
+                tokens = slice(i * P, (i + 1) * P)
+                latent = psum2.tile([P, RANK], F32)
+                nc.tensor.matmul_mx(
+                    out=latent[:],
+                    lhsT=x_codes[:, tokens].bitcast(FP8X4),
+                    lhsT_scale=x_scales[:, tokens],
+                    rhs=w1_codes[:, ROPE_COLS:KV_COLS].bitcast(FP8X4),
+                    rhs_scale=w1_scales[:, ROPE_COLS:KV_COLS],
+                    start=True,
+                    stop=True,
+                )
+                nc.tensor.matmul_mx(
+                    out=k_rope[:, i, :],
+                    lhsT=x_codes[:, tokens].bitcast(FP8X4),
+                    lhsT_scale=x_scales[:, tokens],
+                    rhs=w1_codes[:, 0:ROPE_COLS].bitcast(FP8X4),
+                    rhs_scale=w1_scales[:, 0:ROPE_COLS],
+                    start=True,
+                    stop=True,
+                )
+                nc.vector.scalar_tensor_tensor(
+                    out=c[:, i, :],
+                    in0=latent[:],
+                    scalar=1.0,
+                    in1=b1_bc[:, ROPE_COLS:KV_COLS],
+                    op0=ALU.mult,
+                    op1=ALU.add,
+                    accum_out=sums[:, i : i + 1],
+                )
+            nc.vector.tensor_tensor(
+                out=kv_out[:, :, 0, NOPE_COLS:K_COLS],
+                in0=k_rope[:],
+                in1=b1_bc[:, 0:ROPE_COLS].unsqueeze(1).to_broadcast([P, TILES, ROPE_COLS]),
+                op=ALU.add,
+            )
+
+            neg_mean = small.tile([P, TILES], F32)
+            nc.vector.tensor_scalar_mul(out=neg_mean[:], in0=sums[:], scalar1=-1.0 / RANK)
+            sum_sq = small.tile([P, TILES], F32)
+            for i in range(TILES):
+                squares = work.tile([P, RANK], BF16)
+                nc.scalar.activation(
+                    out=squares[:],
+                    in_=c[:, i, :],
+                    func=ACT.Square,
+                    bias=neg_mean[:, i : i + 1],
+                    scale=1.0,
+                    accum_out=sum_sq[:, i : i + 1],
+                )
+            std = small.tile([P, TILES], F32)
+            nc.scalar.activation(out=std[:], in_=sum_sq[:], func=ACT.Sqrt, bias=eps_col[:], scale=1.0 / RANK)
+            rstd = small.tile([P, TILES], F32)
+            nc.vector.reciprocal(out=rstd[:], in_=std[:])
+            shift = small.tile([P, TILES], F32)
+            nc.vector.tensor_mul(out=shift[:], in0=neg_mean[:], in1=rstd[:])
+            z = work.tile([P, TILES, RANK], F32)
+            for i in range(TILES):
+                nc.scalar.activation(
+                    out=z[:, i, :],
+                    in_=c[:, i, :],
+                    func=ACT.Identity,
+                    bias=shift[:, i : i + 1],
+                    scale=rstd[:, i : i + 1],
+                )
+            return z, kv_out
+
+        def back(g, z, kv_out):
+            cn_planes = work.tile([P, PACK, GROUP], BF16)
+            for t in range(PACK):
+                z_t = psum2.tile([P, TILES, P], F32)
+                for i in range(TILES):
+                    nc.tensor.transpose(z_t[:, i, :], z[:, i, t * P : (t + 1) * P], ident[:])
+                nc.scalar.activation(
+                    out=cn_planes[:, t, :],
+                    in_=z_t[:].rearrange("p i w -> p (i w)"),
+                    func=ACT.Identity,
+                    bias=gb_col[:, PACK + t : PACK + t + 1],
+                    scale=gb_col[:, t : t + 1],
+                )
+            cn_grouped = work.tile([P, GROUP, PACK], BF16, align_bytes=64)
+            regroup(nc, cn_grouped[:], cn_planes[:])
+            cn_codes = work.tile([P, GROUP], U32, align_bytes=64)
+            cn_scales = work.tile([P, GROUP], U8, align_bytes=64)
+            quantise(nc, cn_codes[:], cn_scales[:], cn_grouped[:])
+
+            for i in range(TILES):
+                tokens = slice(i * P, (i + 1) * P)
+                nope_v = psum2.tile([P, 2, NOPE_COLS], F32)
+                nc.tensor.matmul_mx(
+                    out=nope_v[:].rearrange("p s c -> p (s c)"),
+                    lhsT=cn_codes[:, tokens].bitcast(FP8X4),
+                    lhsT_scale=cn_scales[:, tokens],
+                    rhs=w2_codes[:].bitcast(FP8X4),
+                    rhs_scale=w2_scales[:],
+                    start=True,
+                    stop=True,
+                )
+                nc.vector.tensor_tensor(
+                    out=kv_out[:, i, :, 0:NOPE_COLS], in0=nope_v[:], in1=b2_bc[:], op=ALU.add
+                )
+
+            s = g % SEQ_GROUPS
+            table_shape = [P, TILES, HEADS, ROT // 2]
+            cos_g = cos_sb[:, s, :, :].unsqueeze(2).to_broadcast(table_shape)
+            sin_g = sin_sb[:, s, :, :].unsqueeze(2).to_broadcast(table_shape)
+            neg_sin_g = neg_sin_sb[:, s, :, :].unsqueeze(2).to_broadcast(table_shape)
+            pairs = kv_out[:, :, 0, :].rearrange("p i (h e) -> p i h e", h=HEADS)[
+                :, :, :, HEAD - ROT : HEAD
+            ].rearrange("p i h (j e) -> p i h j e", e=2)
+            a = pairs[:, :, :, :, 0]
+            b = pairs[:, :, :, :, 1]
+            by_cos = work.tile([P, 2, TILES, HEADS, ROT // 2], F32)
+            by_sin = work.tile([P, 2, TILES, HEADS, ROT // 2], F32)
+            nc.gpsimd.tensor_tensor(out=by_cos[:, 0], in0=a, in1=cos_g, op=ALU.mult)
+            nc.gpsimd.tensor_tensor(out=by_cos[:, 1], in0=b, in1=cos_g, op=ALU.mult)
+            nc.gpsimd.tensor_tensor(out=by_sin[:, 0], in0=b, in1=neg_sin_g, op=ALU.mult)
+            nc.gpsimd.tensor_tensor(out=by_sin[:, 1], in0=a, in1=sin_g, op=ALU.mult)
+            nc.gpsimd.tensor_tensor(
+                out=pairs,
+                in0=by_cos[:].rearrange("p e i h j -> p i h j e"),
+                in1=by_sin[:].rearrange("p e i h j -> p i h j e"),
+                op=ALU.add,
+            )
+
+            rows = slice(g * GROUP, (g + 1) * GROUP)
+            nc.sync.dma_start(
+                out=k_rows[rows, :].rearrange("(p i) c -> p i c", i=TILES), in_=kv_out[:, :, 0, :]
+            )
+            nc.sync.dma_start(
+                out=v_rows[rows, :].rearrange("(p i) c -> p i c", i=TILES), in_=kv_out[:, :, 1, 0:V_COLS]
+            )
+
+        x_next = x_first
+        pending = None
+        for g in range(GROUPS):
+            x_sb = x_next
+            if g + 1 < GROUPS:
+                x_next = load_x(g + 1)
+            if pending is not None:
+                back(g - 1, pending[0], pending[1])
+            pending = front(g, x_sb)
+        back(GROUPS - 1, pending[0], pending[1])

@@ -59,54 +59,61 @@ def tile_mla_pa_t_kernel(
 
     with ExitStack() as ctx:
         consts = ctx.enter_context(tc.tile_pool(name="consts", bufs=1))
-        xin = ctx.enter_context(tc.tile_pool(name="xin", bufs=3))
+        xin = ctx.enter_context(tc.tile_pool(name="xin", bufs=4))
         work = ctx.enter_context(tc.tile_pool(name="work", bufs=2))
-        small = ctx.enter_context(tc.tile_pool(name="small", bufs=3))
-        outs = ctx.enter_context(tc.tile_pool(name="outs", bufs=3))
+        small = ctx.enter_context(tc.tile_pool(name="small", bufs=4))
+        outs = ctx.enter_context(tc.tile_pool(name="outs", bufs=4))
         psum1 = ctx.enter_context(tc.psum_pool(name="psum1", bufs=1))
         psum2 = ctx.enter_context(tc.psum_pool(name="psum2", bufs=2))
+        ctx.enter_context(tc.manual_schedule())
+
+        x_sb, x_grouped, x_codes, x_scales = {}, {}, {}, {}
+        latent, k_rope, c, sums, sum_sq, rstd, shift, z = {}, {}, {}, {}, {}, {}, {}, {}
+        cn_planes, cn_codes, cn_scales, nope_v, kv_out = {}, {}, {}, {}, {}
+
+        def live(g):
+            return 0 <= g < GROUPS
 
         def load_x(g):
-            x_sb = xin.tile([P, TILES, DIM], BF16)
+            x_tile = xin.tile([P, TILES, DIM], BF16)
             nc.sync.dma_start(
-                out=x_sb[:],
+                out=x_tile[:],
                 in_=x_rows[g * GROUP : (g + 1) * GROUP, :].rearrange("(p i) d -> p i d", i=TILES),
             )
-            return x_sb
+            x_sb[g] = x_tile
 
-        x_first = load_x(0)
-
+        load_x(0)
         w1_raw = consts.tile([P, 2, 2, KV_COLS], BF16)
         nc.sync.dma_start(out=w1_raw[:], in_=wkv_a_w.rearrange("(u q e) c -> q u e c", u=2, e=2))
+        load_x(1)
         w2_raw = consts.tile([P, PACK, NOPE_COLS + V_COLS], BF16)
         nc.sync.dma_start(out=w2_raw[:, :, 0:NOPE_COLS], in_=wk_w.rearrange("(t p) n -> p t n", p=P))
         nc.sync.dma_start(out=w2_raw[:, :, NOPE_COLS:], in_=wv_w.rearrange("(t p) n -> p t n", p=P))
 
+        ident = consts.tile([P, P], F32)
+        make_identity(nc, ident[:])
+
+        eps_col = consts.tile([P, 1], F32)
+        nc.vector.memset(eps_col[:], EPS)
+        gb_rows = consts.tile([P, P], BF16)
+        nc.vector.memset(gb_rows[:], 0.0)
+
         b1_bc = consts.tile([P, KV_COLS], BF16)
         nc.scalar.dma_start(out=b1_bc[:], in_=wkv_a_b.partition_broadcast(P))
+        nc.scalar.dma_start(out=gb_rows[0:PACK, :], in_=kvn_g.rearrange("(t p) -> t p", p=P))
+        nc.scalar.dma_start(out=gb_rows[PACK : 2 * PACK, :], in_=kvn_b.rearrange("(t p) -> t p", p=P))
         b2_bc = consts.tile([P, 2, NOPE_COLS], BF16)
         nc.scalar.dma_start(out=b2_bc[:, 0, :], in_=wk_b.partition_broadcast(P))
         nc.scalar.dma_start(out=b2_bc[:, 1, :], in_=wv_b.partition_broadcast(P))
-
-        gb_rows = consts.tile([P, P], BF16)
-        nc.vector.memset(gb_rows[:], 0.0)
-        nc.scalar.dma_start(out=gb_rows[0:PACK, :], in_=kvn_g.rearrange("(t p) -> t p", p=P))
-        nc.scalar.dma_start(out=gb_rows[PACK : 2 * PACK, :], in_=kvn_b.rearrange("(t p) -> t p", p=P))
-
         cos_sb = consts.tile([P, SEQ_GROUPS, TILES, ROT // 2], BF16)
         nc.scalar.dma_start(out=cos_sb[:], in_=cos.rearrange("(s p i) j -> p s i j", p=P, i=TILES))
         sin_sb = consts.tile([P, SEQ_GROUPS, TILES, ROT // 2], BF16)
         nc.scalar.dma_start(out=sin_sb[:], in_=sin.rearrange("(s p i) j -> p s i j", p=P, i=TILES))
         neg_sin_sb = consts.tile([P, SEQ_GROUPS, TILES, ROT // 2], BF16)
-        nc.vector.tensor_scalar_mul(out=neg_sin_sb[:], in0=sin_sb[:], scalar1=-1.0)
+        nc.gpsimd.tensor_scalar_mul(out=neg_sin_sb[:], in0=sin_sb[:], scalar1=-1.0)
 
-        eps_col = consts.tile([P, 1], F32)
-        nc.vector.memset(eps_col[:], EPS)
         warm = consts.tile([P, 1], F32)
         nc.scalar.activation(out=warm[:], in_=eps_col[:], func=ACT.Sqrt)
-
-        ident = consts.tile([P, P], F32)
-        make_identity(nc, ident[:])
 
         w1_grouped = consts.tile([P, KV_COLS, PACK], BF16, align_bytes=64)
         w1_codes = consts.tile([P, KV_COLS], U32, align_bytes=64)
@@ -118,147 +125,193 @@ def tile_mla_pa_t_kernel(
         w2_grouped = consts.tile([P, NOPE_COLS + V_COLS, PACK], BF16, align_bytes=64)
         w2_codes = consts.tile([P, NOPE_COLS + V_COLS], U32, align_bytes=64)
         w2_scales = consts.tile([P, NOPE_COLS + V_COLS], U8, align_bytes=64)
-        regroup(nc, w2_grouped[:], w2_raw[:])
-        quantise(nc, w2_codes[:], w2_scales[:], w2_grouped[:])
-
-        gb_f32 = consts.tile([P, P], F32)
-        nc.vector.tensor_copy(out=gb_f32[:], in_=gb_rows[:])
-        gb_t = psum2.tile([P, TILES, P], F32, tag="z_t")
-        nc.tensor.transpose(gb_t[:, 0, :], gb_f32[:], ident[:])
         gb_col = consts.tile([P, 2 * PACK], F32)
-        nc.vector.tensor_copy(out=gb_col[:], in_=gb_t[:, 0, 0 : 2 * PACK])
 
-        def front(g, x_sb):
-            x_grouped = work.tile([P, GROUP * PACK], BF16, align_bytes=64)
-            x_grouped_words = x_grouped[:].bitcast(F32)
-            for half in range(2):
-                x_t = psum1.tile([P, 2, 2, P], F32)
-                for i in range(2):
-                    x_words = x_sb[:, 2 * half + i, :].bitcast(F32)
-                    for u in range(2):
-                        nc.tensor.transpose(x_t[:, i, u, :], x_words[:, u * P : (u + 1) * P], ident[:])
-                nc.scalar.copy(
-                    out=x_grouped_words[:, half * GROUP : (half + 1) * GROUP].rearrange(
-                        "p (i w u) -> p i w u", i=2, u=2
-                    ),
-                    in_=x_t[:].rearrange("p i u w -> p i w u"),
-                )
-            x_codes = work.tile([P, GROUP], U32, align_bytes=64)
-            x_scales = work.tile([P, GROUP], U8, align_bytes=64)
-            nc.vector.quantize_mx(out=x_codes[:].bitcast(FP8X4), scales=x_scales[:], in_=x_grouped[:])
+        def prepare_second_stage():
+            regroup(nc, w2_grouped[:], w2_raw[:])
+            quantise(nc, w2_codes[:], w2_scales[:], w2_grouped[:])
+            gb_f32 = consts.tile([P, P], F32)
+            nc.vector.tensor_copy(out=gb_f32[:], in_=gb_rows[:])
+            gb_t = psum2.tile([P, TILES, P], F32, tag="z_t")
+            nc.tensor.transpose(gb_t[:, 0, :], gb_f32[:], ident[:])
+            nc.vector.tensor_copy(out=gb_col[:], in_=gb_t[:, 0, 0 : 2 * PACK])
 
-            kv_out = outs.tile([P, TILES, 2, K_COLS], F32)
-            c = work.tile([P, TILES, RANK], F32)
-            sums = small.tile([P, TILES], F32)
-            k_rope = psum1.tile([P, TILES, ROPE_COLS], F32)
-            for i in range(TILES):
-                tokens = slice(i * P, (i + 1) * P)
-                latent = psum2.tile([P, RANK], F32)
+        def transpose_x(g, half):
+            x_t = psum1.tile([P, 2, 2, P], F32)
+            for i in range(2):
+                x_words = x_sb[g][:, 2 * half + i, :].bitcast(F32)
+                for u in range(2):
+                    nc.tensor.transpose(x_t[:, i, u, :], x_words[:, u * P : (u + 1) * P], ident[:])
+            return x_t
+
+        def copy_x(g, half, x_t):
+            if half == 0:
+                grouped_tile = work.tile([P, GROUP * PACK], BF16, align_bytes=64)
+                x_grouped[g] = grouped_tile
+            nc.scalar.copy(
+                out=x_grouped[g][:]
+                .bitcast(F32)[:, half * GROUP : (half + 1) * GROUP]
+                .rearrange("p (i w u) -> p i w u", i=2, u=2),
+                in_=x_t[:].rearrange("p i u w -> p i w u"),
+            )
+
+        def quantise_x(g, half):
+            if half == 0:
+                codes_tile = work.tile([P, GROUP], U32, align_bytes=64)
+                scales_tile = work.tile([P, GROUP], U8, align_bytes=64)
+                x_codes[g], x_scales[g] = codes_tile, scales_tile
+            cols = slice(half * 2 * P, (half + 1) * 2 * P)
+            nc.vector.quantize_mx(
+                out=x_codes[g][:, cols].bitcast(FP8X4),
+                scales=x_scales[g][:, cols],
+                in_=x_grouped[g][:, half * 2 * P * PACK : (half + 1) * 2 * P * PACK],
+            )
+
+        def project_kv(g, i):
+            if i == 0:
+                rope_bank = psum1.tile([P, TILES, ROPE_COLS], F32)
+                k_rope[g] = rope_bank
+            tokens = slice(i * P, (i + 1) * P)
+            latent_bank = psum2.tile([P, RANK], F32)
+            latent[g, i] = latent_bank
+            for out, cols in (
+                (latent_bank[:], slice(ROPE_COLS, KV_COLS)),
+                (k_rope[g][:, i, :], slice(0, ROPE_COLS)),
+            ):
                 nc.tensor.matmul_mx(
-                    out=latent[:],
-                    lhsT=x_codes[:, tokens].bitcast(FP8X4),
-                    lhsT_scale=x_scales[:, tokens],
-                    rhs=w1_codes[:, ROPE_COLS:KV_COLS].bitcast(FP8X4),
-                    rhs_scale=w1_scales[:, ROPE_COLS:KV_COLS],
+                    out=out,
+                    lhsT=x_codes[g][:, tokens].bitcast(FP8X4),
+                    lhsT_scale=x_scales[g][:, tokens],
+                    rhs=w1_codes[:, cols].bitcast(FP8X4),
+                    rhs_scale=w1_scales[:, cols],
                     start=True,
                     stop=True,
                 )
-                nc.tensor.matmul_mx(
-                    out=k_rope[:, i, :],
-                    lhsT=x_codes[:, tokens].bitcast(FP8X4),
-                    lhsT_scale=x_scales[:, tokens],
-                    rhs=w1_codes[:, 0:ROPE_COLS].bitcast(FP8X4),
-                    rhs_scale=w1_scales[:, 0:ROPE_COLS],
-                    start=True,
-                    stop=True,
-                )
-                nc.vector.scalar_tensor_tensor(
-                    out=c[:, i, :],
-                    in0=latent[:],
-                    scalar=1.0,
-                    in1=b1_bc[:, ROPE_COLS:KV_COLS],
-                    op0=ALU.mult,
-                    op1=ALU.add,
-                    accum_out=sums[:, i : i + 1],
-                )
+
+        def add_bias_and_sum(g, i):
+            if i == 0:
+                c_tile = work.tile([P, TILES, RANK], F32)
+                sums_tile = small.tile([P, TILES], F32)
+                c[g], sums[g] = c_tile, sums_tile
+            nc.vector.scalar_tensor_tensor(
+                out=c[g][:, i, :],
+                in0=latent[g, i][:],
+                scalar=1.0,
+                in1=b1_bc[:, ROPE_COLS:KV_COLS],
+                op0=ALU.mult,
+                op1=ALU.add,
+                accum_out=sums[g][:, i : i + 1],
+            )
+
+        def sum_squares(g, i):
+            if i == 0:
+                sum_sq_tile = small.tile([P, TILES], F32)
+                sum_sq[g] = sum_sq_tile
+            squares = work.tile([P, RANK], BF16)
+            nc.scalar.activation(
+                out=squares[:],
+                in_=c[g][:, i, :],
+                func=ACT.Square,
+                bias=sums[g][:, i : i + 1],
+                scale=-1.0 * RANK,
+                accum_out=sum_sq[g][:, i : i + 1],
+            )
+
+        def std_dev(g):
+            std = small.tile([P, TILES], F32)
+            nc.scalar.activation(
+                out=std[:], in_=sum_sq[g][:], func=ACT.Sqrt, bias=eps_col[:], scale=1.0 / RANK**3
+            )
+            return std
+
+        def rstd_and_shift(g, std):
+            rstd_tile = small.tile([P, TILES], F32)
+            shift_tile = small.tile([P, TILES], F32)
+            rstd[g], shift[g] = rstd_tile, shift_tile
+            nc.vector.reciprocal(out=rstd_tile[:], in_=std[:])
+            nc.vector.scalar_tensor_tensor(
+                out=shift_tile[:],
+                in0=sums[g][:],
+                scalar=-1.0 / RANK,
+                in1=rstd_tile[:],
+                op0=ALU.mult,
+                op1=ALU.mult,
+            )
+
+        def add_rope_bias(g):
+            kv_tile = outs.tile([P, TILES, 2, K_COLS], F32)
+            kv_out[g] = kv_tile
             nc.vector.tensor_tensor(
-                out=kv_out[:, :, 0, NOPE_COLS:K_COLS],
-                in0=k_rope[:],
+                out=kv_tile[:, :, 0, NOPE_COLS:K_COLS],
+                in0=k_rope[g][:],
                 in1=b1_bc[:, 0:ROPE_COLS].unsqueeze(1).to_broadcast([P, TILES, ROPE_COLS]),
                 op=ALU.add,
             )
 
-            neg_mean = small.tile([P, TILES], F32)
-            nc.vector.tensor_scalar_mul(out=neg_mean[:], in0=sums[:], scalar1=-1.0 / RANK)
-            sum_sq = small.tile([P, TILES], F32)
-            for i in range(TILES):
-                squares = work.tile([P, RANK], BF16)
-                nc.scalar.activation(
-                    out=squares[:],
-                    in_=c[:, i, :],
-                    func=ACT.Square,
-                    bias=neg_mean[:, i : i + 1],
-                    scale=1.0,
-                    accum_out=sum_sq[:, i : i + 1],
-                )
-            std = small.tile([P, TILES], F32)
-            nc.scalar.activation(out=std[:], in_=sum_sq[:], func=ACT.Sqrt, bias=eps_col[:], scale=1.0 / RANK)
-            rstd = small.tile([P, TILES], F32)
-            nc.vector.reciprocal(out=rstd[:], in_=std[:])
-            shift = small.tile([P, TILES], F32)
-            nc.vector.tensor_mul(out=shift[:], in0=neg_mean[:], in1=rstd[:])
-            z = work.tile([P, TILES, RANK], F32)
-            for i in range(TILES):
-                nc.scalar.activation(
-                    out=z[:, i, :],
-                    in_=c[:, i, :],
-                    func=ACT.Identity,
-                    bias=shift[:, i : i + 1],
-                    scale=rstd[:, i : i + 1],
-                )
-            return z, kv_out
+        def normalise(g, i):
+            if i == 0:
+                z_tile = work.tile([P, TILES, RANK], F32)
+                z[g] = z_tile
+            nc.scalar.activation(
+                out=z[g][:, i, :],
+                in_=c[g][:, i, :],
+                func=ACT.Identity,
+                bias=shift[g][:, i : i + 1],
+                scale=rstd[g][:, i : i + 1],
+            )
 
-        def back(g, z, kv_out):
-            cn_planes = work.tile([P, PACK, GROUP], BF16)
-            for t in range(PACK):
-                z_t = psum2.tile([P, TILES, P], F32)
-                for i in range(TILES):
-                    nc.tensor.transpose(z_t[:, i, :], z[:, i, t * P : (t + 1) * P], ident[:])
-                nc.scalar.activation(
-                    out=cn_planes[:, t, :],
-                    in_=z_t[:].rearrange("p i w -> p (i w)"),
-                    func=ACT.Identity,
-                    bias=gb_col[:, PACK + t : PACK + t + 1],
-                    scale=gb_col[:, t : t + 1],
-                )
+        def transpose_z(g, t):
+            z_t = psum2.tile([P, TILES, P], F32)
+            for i in range(TILES):
+                nc.tensor.transpose(z_t[:, i, :], z[g][:, i, t * P : (t + 1) * P], ident[:])
+            return z_t
+
+        def gain_and_bias(g, t, z_t):
+            if t == 0:
+                planes_tile = work.tile([P, PACK, GROUP], BF16)
+                cn_planes[g] = planes_tile
+            nc.scalar.activation(
+                out=cn_planes[g][:, t, :],
+                in_=z_t[:].rearrange("p i w -> p (i w)"),
+                func=ACT.Identity,
+                bias=gb_col[:, PACK + t : PACK + t + 1],
+                scale=gb_col[:, t : t + 1],
+            )
+
+        def quantise_cn(g):
             cn_grouped = work.tile([P, GROUP, PACK], BF16, align_bytes=64)
-            regroup(nc, cn_grouped[:], cn_planes[:])
-            cn_codes = work.tile([P, GROUP], U32, align_bytes=64)
-            cn_scales = work.tile([P, GROUP], U8, align_bytes=64)
-            quantise(nc, cn_codes[:], cn_scales[:], cn_grouped[:])
+            regroup(nc, cn_grouped[:], cn_planes[g][:])
+            cn_codes_tile = work.tile([P, GROUP], U32, align_bytes=64)
+            cn_scales_tile = work.tile([P, GROUP], U8, align_bytes=64)
+            cn_codes[g], cn_scales[g] = cn_codes_tile, cn_scales_tile
+            quantise(nc, cn_codes_tile[:], cn_scales_tile[:], cn_grouped[:])
 
-            for i in range(TILES):
-                tokens = slice(i * P, (i + 1) * P)
-                nope_v = psum2.tile([P, 2, NOPE_COLS], F32)
-                nc.tensor.matmul_mx(
-                    out=nope_v[:].rearrange("p s c -> p (s c)"),
-                    lhsT=cn_codes[:, tokens].bitcast(FP8X4),
-                    lhsT_scale=cn_scales[:, tokens],
-                    rhs=w2_codes[:].bitcast(FP8X4),
-                    rhs_scale=w2_scales[:],
-                    start=True,
-                    stop=True,
-                )
-                nc.vector.tensor_tensor(
-                    out=kv_out[:, i, :, 0:NOPE_COLS], in0=nope_v[:], in1=b2_bc[:], op=ALU.add
-                )
+        def project_out(g, i):
+            tokens = slice(i * P, (i + 1) * P)
+            out_bank = psum2.tile([P, 2, NOPE_COLS], F32)
+            nope_v[g, i] = out_bank
+            nc.tensor.matmul_mx(
+                out=out_bank[:].rearrange("p s c -> p (s c)"),
+                lhsT=cn_codes[g][:, tokens].bitcast(FP8X4),
+                lhsT_scale=cn_scales[g][:, tokens],
+                rhs=w2_codes[:].bitcast(FP8X4),
+                rhs_scale=w2_scales[:],
+                start=True,
+                stop=True,
+            )
 
+        def add_out_bias(g, i):
+            nc.vector.tensor_tensor(
+                out=kv_out[g][:, i, :, 0:NOPE_COLS], in0=nope_v[g, i][:], in1=b2_bc[:], op=ALU.add
+            )
+
+        def rotate(g):
             s = g % SEQ_GROUPS
             table_shape = [P, TILES, HEADS, ROT // 2]
             cos_g = cos_sb[:, s, :, :].unsqueeze(2).to_broadcast(table_shape)
             sin_g = sin_sb[:, s, :, :].unsqueeze(2).to_broadcast(table_shape)
             neg_sin_g = neg_sin_sb[:, s, :, :].unsqueeze(2).to_broadcast(table_shape)
-            pairs = kv_out[:, :, 0, :].rearrange("p i (h e) -> p i h e", h=HEADS)[
+            pairs = kv_out[g][:, :, 0, :].rearrange("p i (h e) -> p i h e", h=HEADS)[
                 :, :, :, HEAD - ROT : HEAD
             ].rearrange("p i h (j e) -> p i h j e", e=2)
             a = pairs[:, :, :, :, 0]
@@ -276,21 +329,62 @@ def tile_mla_pa_t_kernel(
                 op=ALU.add,
             )
 
+        def store(g):
             rows = slice(g * GROUP, (g + 1) * GROUP)
             nc.sync.dma_start(
-                out=k_rows[rows, :].rearrange("(p i) c -> p i c", i=TILES), in_=kv_out[:, :, 0, :]
+                out=v_rows[rows, :].rearrange("(p i) c -> p i c", i=TILES),
+                in_=kv_out[g][:, :, 1, 0:V_COLS],
             )
             nc.sync.dma_start(
-                out=v_rows[rows, :].rearrange("(p i) c -> p i c", i=TILES), in_=kv_out[:, :, 1, 0:V_COLS]
+                out=k_rows[rows, :].rearrange("(p i) c -> p i c", i=TILES), in_=kv_out[g][:, :, 0, :]
             )
 
-        x_next = x_first
-        pending = None
-        for g in range(GROUPS):
-            x_sb = x_next
-            if g + 1 < GROUPS:
-                x_next = load_x(g + 1)
-            if pending is not None:
-                back(g - 1, pending[0], pending[1])
-            pending = front(g, x_sb)
-        back(GROUPS - 1, pending[0], pending[1])
+        def iteration(k):
+            if live(k):
+                for i in range(TILES):
+                    add_bias_and_sum(k, i)
+                    sum_squares(k, i)
+                    if i + 2 < TILES:
+                        project_kv(k, i + 2)
+                std = std_dev(k)
+            if live(k + 1):
+                x_t = transpose_x(k + 1, 0)
+                copy_x(k + 1, 0, x_t)
+                x_t = transpose_x(k + 1, 1)
+            if live(k - 2):
+                quantise_cn(k - 2)
+                project_out(k - 2, 0)
+                project_out(k - 2, 1)
+            if live(k + 1):
+                quantise_x(k + 1, 0)
+            if live(k):
+                add_rope_bias(k)
+                rstd_and_shift(k, std)
+            if live(k + 1):
+                project_kv(k + 1, 0)
+                project_kv(k + 1, 1)
+            if live(k - 1):
+                for i in range(TILES):
+                    normalise(k - 1, i)
+            if live(k + 1):
+                copy_x(k + 1, 1, x_t)
+            for t in range(PACK):
+                if live(k - 2):
+                    add_out_bias(k - 2, t)
+                    if t + 2 < TILES:
+                        project_out(k - 2, t + 2)
+                if live(k - 1):
+                    z_t = transpose_z(k - 1, t)
+                    gain_and_bias(k - 1, t, z_t)
+            if live(k + 1):
+                quantise_x(k + 1, 1)
+            if live(k + 3):
+                load_x(k + 3)
+            if live(k - 2):
+                rotate(k - 2)
+                store(k - 2)
+
+        iteration(-1)
+        prepare_second_stage()
+        for k in range(GROUPS + 2):
+            iteration(k)

@@ -63,16 +63,14 @@ def tile_mla_pa_t_kernel(
         work = ctx.enter_context(tc.tile_pool(name="work", bufs=2))
         small = ctx.enter_context(tc.tile_pool(name="small", bufs=4))
         outs = ctx.enter_context(tc.tile_pool(name="outs", bufs=4))
-        psum1 = ctx.enter_context(tc.psum_pool(name="psum1", bufs=1))
-        psum2 = ctx.enter_context(tc.psum_pool(name="psum2", bufs=2))
+        psum_s = ctx.enter_context(tc.psum_pool(name="psum_s", bufs=3))
+        psum_v = ctx.enter_context(tc.psum_pool(name="psum_v", bufs=4))
+        psum_r = ctx.enter_context(tc.psum_pool(name="psum_r", bufs=1))
         ctx.enter_context(tc.manual_schedule())
 
-        x_sb, x_grouped, x_codes, x_scales = {}, {}, {}, {}
-        latent, k_rope, c, sums, sum_sq, rstd, shift, z = {}, {}, {}, {}, {}, {}, {}, {}
-        cn_planes, cn_codes, cn_scales, nope_v, kv_out = {}, {}, {}, {}, {}
-
-        def live(g):
-            return 0 <= g < GROUPS
+        x_sb, x_t, x_grouped, x_codes, x_scales = {}, {}, {}, {}, {}
+        latent, k_rope, c, sums, sum_sq, std, rstd, shift, z, z_t = {}, {}, {}, {}, {}, {}, {}, {}, {}, {}
+        cn_planes, cn_grouped, cn_codes, cn_scales, nope_v, kv_out = {}, {}, {}, {}, {}, {}
 
         def load_x(g):
             x_tile = xin.tile([P, TILES, DIM], BF16)
@@ -128,23 +126,23 @@ def tile_mla_pa_t_kernel(
         gb_col = consts.tile([P, 2 * PACK], F32)
 
         def prepare_second_stage():
-            regroup(nc, w2_grouped[:], w2_raw[:])
-            quantise(nc, w2_codes[:], w2_scales[:], w2_grouped[:])
             gb_f32 = consts.tile([P, P], F32)
             nc.vector.tensor_copy(out=gb_f32[:], in_=gb_rows[:])
-            gb_t = psum2.tile([P, TILES, P], F32, tag="z_t")
+            gb_t = psum_s.tile([P, TILES, P], F32, tag="to_scalar")
             nc.tensor.transpose(gb_t[:, 0, :], gb_f32[:], ident[:])
+            regroup(nc, w2_grouped[:], w2_raw[:])
             nc.vector.tensor_copy(out=gb_col[:], in_=gb_t[:, 0, 0 : 2 * PACK])
+            quantise(nc, w2_codes[:], w2_scales[:], w2_grouped[:])
 
         def transpose_x(g, half):
-            x_t = psum1.tile([P, 2, 2, P], F32)
+            x_bank = psum_s.tile([P, 2, 2, P], F32, tag="to_scalar")
+            x_t[g, half] = x_bank
             for i in range(2):
                 x_words = x_sb[g][:, 2 * half + i, :].bitcast(F32)
                 for u in range(2):
-                    nc.tensor.transpose(x_t[:, i, u, :], x_words[:, u * P : (u + 1) * P], ident[:])
-            return x_t
+                    nc.tensor.transpose(x_bank[:, i, u, :], x_words[:, u * P : (u + 1) * P], ident[:])
 
-        def copy_x(g, half, x_t):
+        def copy_x(g, half):
             if half == 0:
                 grouped_tile = work.tile([P, GROUP * PACK], BF16, align_bytes=64)
                 x_grouped[g] = grouped_tile
@@ -152,7 +150,7 @@ def tile_mla_pa_t_kernel(
                 out=x_grouped[g][:]
                 .bitcast(F32)[:, half * GROUP : (half + 1) * GROUP]
                 .rearrange("p (i w u) -> p i w u", i=2, u=2),
-                in_=x_t[:].rearrange("p i u w -> p i w u"),
+                in_=x_t[g, half][:].rearrange("p i u w -> p i w u"),
             )
 
         def quantise_x(g, half):
@@ -169,10 +167,10 @@ def tile_mla_pa_t_kernel(
 
         def project_kv(g, i):
             if i == 0:
-                rope_bank = psum1.tile([P, TILES, ROPE_COLS], F32)
+                rope_bank = psum_r.tile([P, TILES, ROPE_COLS], F32)
                 k_rope[g] = rope_bank
             tokens = slice(i * P, (i + 1) * P)
-            latent_bank = psum2.tile([P, RANK], F32)
+            latent_bank = psum_v.tile([P, RANK], F32, tag="to_vector")
             latent[g, i] = latent_bank
             for out, cols in (
                 (latent_bank[:], slice(ROPE_COLS, KV_COLS)),
@@ -218,17 +216,17 @@ def tile_mla_pa_t_kernel(
             )
 
         def std_dev(g):
-            std = small.tile([P, TILES], F32)
+            std_tile = small.tile([P, TILES], F32)
+            std[g] = std_tile
             nc.scalar.activation(
-                out=std[:], in_=sum_sq[g][:], func=ACT.Sqrt, bias=eps_col[:], scale=1.0 / RANK**3
+                out=std_tile[:], in_=sum_sq[g][:], func=ACT.Sqrt, bias=eps_col[:], scale=1.0 / RANK**3
             )
-            return std
 
-        def rstd_and_shift(g, std):
+        def rstd_and_shift(g):
             rstd_tile = small.tile([P, TILES], F32)
             shift_tile = small.tile([P, TILES], F32)
             rstd[g], shift[g] = rstd_tile, shift_tile
-            nc.vector.reciprocal(out=rstd_tile[:], in_=std[:])
+            nc.vector.reciprocal(out=rstd_tile[:], in_=std[g][:])
             nc.vector.scalar_tensor_tensor(
                 out=shift_tile[:],
                 in0=sums[g][:],
@@ -261,34 +259,37 @@ def tile_mla_pa_t_kernel(
             )
 
         def transpose_z(g, t):
-            z_t = psum2.tile([P, TILES, P], F32)
+            z_bank = psum_s.tile([P, TILES, P], F32, tag="to_scalar")
+            z_t[g, t] = z_bank
             for i in range(TILES):
-                nc.tensor.transpose(z_t[:, i, :], z[g][:, i, t * P : (t + 1) * P], ident[:])
-            return z_t
+                nc.tensor.transpose(z_bank[:, i, :], z[g][:, i, t * P : (t + 1) * P], ident[:])
 
-        def gain_and_bias(g, t, z_t):
+        def gain_and_bias(g, t):
             if t == 0:
                 planes_tile = work.tile([P, PACK, GROUP], BF16)
                 cn_planes[g] = planes_tile
             nc.scalar.activation(
                 out=cn_planes[g][:, t, :],
-                in_=z_t[:].rearrange("p i w -> p (i w)"),
+                in_=z_t[g, t][:].rearrange("p i w -> p (i w)"),
                 func=ACT.Identity,
                 bias=gb_col[:, PACK + t : PACK + t + 1],
                 scale=gb_col[:, t : t + 1],
             )
 
+        def regroup_cn(g):
+            cn_grouped_tile = work.tile([P, GROUP, PACK], BF16, align_bytes=64)
+            cn_grouped[g] = cn_grouped_tile
+            regroup(nc, cn_grouped_tile[:], cn_planes[g][:])
+
         def quantise_cn(g):
-            cn_grouped = work.tile([P, GROUP, PACK], BF16, align_bytes=64)
-            regroup(nc, cn_grouped[:], cn_planes[g][:])
             cn_codes_tile = work.tile([P, GROUP], U32, align_bytes=64)
             cn_scales_tile = work.tile([P, GROUP], U8, align_bytes=64)
             cn_codes[g], cn_scales[g] = cn_codes_tile, cn_scales_tile
-            quantise(nc, cn_codes_tile[:], cn_scales_tile[:], cn_grouped[:])
+            quantise(nc, cn_codes_tile[:], cn_scales_tile[:], cn_grouped[g][:])
 
         def project_out(g, i):
             tokens = slice(i * P, (i + 1) * P)
-            out_bank = psum2.tile([P, 2, NOPE_COLS], F32)
+            out_bank = psum_v.tile([P, 2, NOPE_COLS], F32, tag="to_vector")
             nope_v[g, i] = out_bank
             nc.tensor.matmul_mx(
                 out=out_bank[:].rearrange("p s c -> p (s c)"),
@@ -305,19 +306,20 @@ def tile_mla_pa_t_kernel(
                 out=kv_out[g][:, i, :, 0:NOPE_COLS], in0=nope_v[g, i][:], in1=b2_bc[:], op=ALU.add
             )
 
-        def rotate(g):
+        def rotate(g, half):
             s = g % SEQ_GROUPS
-            table_shape = [P, TILES, HEADS, ROT // 2]
-            cos_g = cos_sb[:, s, :, :].unsqueeze(2).to_broadcast(table_shape)
-            sin_g = sin_sb[:, s, :, :].unsqueeze(2).to_broadcast(table_shape)
-            neg_sin_g = neg_sin_sb[:, s, :, :].unsqueeze(2).to_broadcast(table_shape)
-            pairs = kv_out[g][:, :, 0, :].rearrange("p i (h e) -> p i h e", h=HEADS)[
+            tiles = slice(2 * half, 2 * half + 2)
+            table_shape = [P, 2, HEADS, ROT // 2]
+            cos_g = cos_sb[:, s, tiles, :].unsqueeze(2).to_broadcast(table_shape)
+            sin_g = sin_sb[:, s, tiles, :].unsqueeze(2).to_broadcast(table_shape)
+            neg_sin_g = neg_sin_sb[:, s, tiles, :].unsqueeze(2).to_broadcast(table_shape)
+            pairs = kv_out[g][:, tiles, 0, :].rearrange("p i (h e) -> p i h e", h=HEADS)[
                 :, :, :, HEAD - ROT : HEAD
             ].rearrange("p i h (j e) -> p i h j e", e=2)
             a = pairs[:, :, :, :, 0]
             b = pairs[:, :, :, :, 1]
-            by_cos = work.tile([P, 2, TILES, HEADS, ROT // 2], F32)
-            by_sin = work.tile([P, 2, TILES, HEADS, ROT // 2], F32)
+            by_cos = work.tile([P, 2, 2, HEADS, ROT // 2], F32)
+            by_sin = work.tile([P, 2, 2, HEADS, ROT // 2], F32)
             nc.gpsimd.tensor_tensor(out=by_cos[:, 0], in0=a, in1=cos_g, op=ALU.mult)
             nc.gpsimd.tensor_tensor(out=by_cos[:, 1], in0=b, in1=cos_g, op=ALU.mult)
             nc.gpsimd.tensor_tensor(out=by_sin[:, 0], in0=b, in1=neg_sin_g, op=ALU.mult)
@@ -329,62 +331,74 @@ def tile_mla_pa_t_kernel(
                 op=ALU.add,
             )
 
-        def store(g):
-            rows = slice(g * GROUP, (g + 1) * GROUP)
+        def store_k(g, half):
+            tiles = slice(2 * half, 2 * half + 2)
             nc.sync.dma_start(
-                out=v_rows[rows, :].rearrange("(p i) c -> p i c", i=TILES),
+                out=k_rows[g * GROUP : (g + 1) * GROUP, :].rearrange("(p i) c -> p i c", i=TILES)[:, tiles, :],
+                in_=kv_out[g][:, tiles, 0, :],
+            )
+
+        def store_v(g):
+            nc.sync.dma_start(
+                out=v_rows[g * GROUP : (g + 1) * GROUP, :].rearrange("(p i) c -> p i c", i=TILES),
                 in_=kv_out[g][:, :, 1, 0:V_COLS],
             )
-            nc.sync.dma_start(
-                out=k_rows[rows, :].rearrange("(p i) c -> p i c", i=TILES), in_=kv_out[g][:, :, 0, :]
-            )
+
+        def run(g, step, *args):
+            if 0 <= g < GROUPS:
+                step(g, *args)
 
         def iteration(k):
-            if live(k):
-                for i in range(TILES):
-                    add_bias_and_sum(k, i)
-                    sum_squares(k, i)
-                    if i + 2 < TILES:
-                        project_kv(k, i + 2)
-                std = std_dev(k)
-            if live(k + 1):
-                x_t = transpose_x(k + 1, 0)
-                copy_x(k + 1, 0, x_t)
-                x_t = transpose_x(k + 1, 1)
-            if live(k - 2):
-                quantise_cn(k - 2)
-                project_out(k - 2, 0)
-                project_out(k - 2, 1)
-            if live(k + 1):
-                quantise_x(k + 1, 0)
-            if live(k):
-                add_rope_bias(k)
-                rstd_and_shift(k, std)
-            if live(k + 1):
-                project_kv(k + 1, 0)
-                project_kv(k + 1, 1)
-            if live(k - 1):
-                for i in range(TILES):
-                    normalise(k - 1, i)
-            if live(k + 1):
-                copy_x(k + 1, 1, x_t)
-            for t in range(PACK):
-                if live(k - 2):
-                    add_out_bias(k - 2, t)
-                    if t + 2 < TILES:
-                        project_out(k - 2, t + 2)
-                if live(k - 1):
-                    z_t = transpose_z(k - 1, t)
-                    gain_and_bias(k - 1, t, z_t)
-            if live(k + 1):
-                quantise_x(k + 1, 1)
-            if live(k + 3):
-                load_x(k + 3)
-            if live(k - 2):
-                rotate(k - 2)
-                store(k - 2)
+            run(k + 4, load_x)
+            run(k + 1, quantise_x, 1)
+            run(k + 1, project_kv, 2)
+            run(k + 1, project_kv, 3)
+            run(k + 1, add_bias_and_sum, 0)
+            run(k - 1, regroup_cn)
+            for i in range(TILES):
+                run(k, normalise, i)
+            run(k, transpose_z, 0)
+            run(k, transpose_z, 1)
+            run(k + 2, transpose_x, 0)
+            run(k + 1, sum_squares, 0)
+            run(k + 1, add_bias_and_sum, 1)
+            run(k + 1, sum_squares, 1)
+            run(k - 1, quantise_cn)
+            run(k - 1, project_out, 0)
+            run(k - 1, project_out, 1)
+            run(k, gain_and_bias, 0)
+            run(k, gain_and_bias, 1)
+            run(k + 2, copy_x, 0)
+            run(k, transpose_z, 2)
+            run(k + 2, transpose_x, 1)
+            run(k + 1, add_bias_and_sum, 2)
+            run(k + 1, sum_squares, 2)
+            run(k - 1, project_out, 2)
+            run(k, transpose_z, 3)
+            run(k + 1, add_bias_and_sum, 3)
+            run(k + 1, sum_squares, 3)
+            run(k - 1, project_out, 3)
+            run(k + 1, std_dev)
+            run(k + 1, add_rope_bias)
+            run(k - 1, add_out_bias, 0)
+            run(k + 2, quantise_x, 0)
+            run(k + 2, project_kv, 0)
+            run(k - 1, add_out_bias, 1)
+            run(k + 2, project_kv, 1)
+            run(k - 1, rotate, 0)
+            run(k - 1, store_k, 0)
+            run(k + 1, rstd_and_shift)
+            run(k, gain_and_bias, 2)
+            run(k + 2, copy_x, 1)
+            run(k, gain_and_bias, 3)
+            run(k - 1, add_out_bias, 2)
+            run(k - 1, add_out_bias, 3)
+            run(k - 1, store_v)
+            run(k - 1, rotate, 1)
+            run(k - 1, store_k, 1)
 
+        iteration(-2)
         iteration(-1)
         prepare_second_stage()
-        for k in range(GROUPS + 2):
+        for k in range(GROUPS + 1):
             iteration(k)

@@ -307,6 +307,7 @@ def tile_mla_pa_t_kernel(
             )
 
         def rotate(g, half):
+            engine = nc.vector if (g == GROUPS - 1 and half == 1) else nc.gpsimd
             s = g % SEQ_GROUPS
             tiles = slice(2 * half, 2 * half + 2)
             table_shape = [P, 2, HEADS, ROT // 2]
@@ -320,11 +321,11 @@ def tile_mla_pa_t_kernel(
             b = pairs[:, :, :, :, 1]
             by_cos = work.tile([P, 2, 2, HEADS, ROT // 2], F32)
             by_sin = work.tile([P, 2, 2, HEADS, ROT // 2], F32)
-            nc.gpsimd.tensor_tensor(out=by_cos[:, 0], in0=a, in1=cos_g, op=ALU.mult)
-            nc.gpsimd.tensor_tensor(out=by_cos[:, 1], in0=b, in1=cos_g, op=ALU.mult)
-            nc.gpsimd.tensor_tensor(out=by_sin[:, 0], in0=b, in1=neg_sin_g, op=ALU.mult)
-            nc.gpsimd.tensor_tensor(out=by_sin[:, 1], in0=a, in1=sin_g, op=ALU.mult)
-            nc.gpsimd.tensor_tensor(
+            engine.tensor_tensor(out=by_cos[:, 0], in0=a, in1=cos_g, op=ALU.mult)
+            engine.tensor_tensor(out=by_cos[:, 1], in0=b, in1=cos_g, op=ALU.mult)
+            engine.tensor_tensor(out=by_sin[:, 0], in0=b, in1=neg_sin_g, op=ALU.mult)
+            engine.tensor_tensor(out=by_sin[:, 1], in0=a, in1=sin_g, op=ALU.mult)
+            engine.tensor_tensor(
                 out=pairs,
                 in0=by_cos[:].rearrange("p e i h j -> p i h j e"),
                 in1=by_sin[:].rearrange("p e i h j -> p i h j e"),
@@ -350,25 +351,23 @@ def tile_mla_pa_t_kernel(
 
         def iteration(k):
             run(k + 4, load_x)
+            run(k + 2, transpose_x, 0)
             run(k + 1, quantise_x, 1)
             run(k + 1, project_kv, 2)
             run(k + 1, project_kv, 3)
-            run(k + 1, add_bias_and_sum, 0)
             run(k - 1, regroup_cn)
+            run(k - 1, quantise_cn)
             for i in range(TILES):
                 run(k, normalise, i)
             run(k, transpose_z, 0)
             run(k, transpose_z, 1)
-            run(k + 2, transpose_x, 0)
-            run(k + 1, sum_squares, 0)
-            run(k + 1, add_bias_and_sum, 1)
-            run(k + 1, sum_squares, 1)
-            run(k - 1, quantise_cn)
-            run(k - 1, project_out, 0)
-            run(k - 1, project_out, 1)
+            run(k + 2, copy_x, 0)
+            for i in range(2):
+                run(k + 1, add_bias_and_sum, i)
+                run(k + 1, sum_squares, i)
+                run(k - 1, project_out, i)
             run(k, gain_and_bias, 0)
             run(k, gain_and_bias, 1)
-            run(k + 2, copy_x, 0)
             run(k, transpose_z, 2)
             run(k + 2, transpose_x, 1)
             run(k + 1, add_bias_and_sum, 2)

@@ -63,6 +63,7 @@ def tile_mla_pa_t_kernel(
         work = ctx.enter_context(tc.tile_pool(name="work", bufs=2))
         small = ctx.enter_context(tc.tile_pool(name="small", bufs=4))
         outs = ctx.enter_context(tc.tile_pool(name="outs", bufs=4))
+        rot = ctx.enter_context(tc.tile_pool(name="rot", bufs=2))
         psum_s = ctx.enter_context(tc.psum_pool(name="psum_s", bufs=3))
         psum_v = ctx.enter_context(tc.psum_pool(name="psum_v", bufs=4))
         psum_r = ctx.enter_context(tc.psum_pool(name="psum_r", bufs=1))
@@ -247,16 +248,26 @@ def tile_mla_pa_t_kernel(
             )
 
         def normalise(g, i):
-            if i == 0:
+            if g not in z:
                 z_tile = work.tile([P, TILES, RANK], F32)
                 z[g] = z_tile
-            nc.scalar.activation(
-                out=z[g][:, i, :],
-                in_=c[g][:, i, :],
-                func=ACT.Identity,
-                bias=shift[g][:, i : i + 1],
-                scale=rstd[g][:, i : i + 1],
-            )
+            if i == TILES - 1:
+                nc.gpsimd.tensor_scalar(
+                    out=z[g][:, i, :],
+                    in0=c[g][:, i, :],
+                    scalar1=rstd[g][:, i : i + 1],
+                    scalar2=shift[g][:, i : i + 1],
+                    op0=ALU.mult,
+                    op1=ALU.add,
+                )
+            else:
+                nc.scalar.activation(
+                    out=z[g][:, i, :],
+                    in_=c[g][:, i, :],
+                    func=ACT.Identity,
+                    bias=shift[g][:, i : i + 1],
+                    scale=rstd[g][:, i : i + 1],
+                )
 
         def transpose_z(g, t):
             z_bank = psum_s.tile([P, TILES, P], F32, tag="to_scalar")
@@ -306,11 +317,10 @@ def tile_mla_pa_t_kernel(
                 out=kv_out[g][:, i, :, 0:NOPE_COLS], in0=nope_v[g, i][:], in1=b2_bc[:], op=ALU.add
             )
 
-        def rotate(g, half):
-            engine = nc.vector if (g == GROUPS - 1 and half == 1) else nc.gpsimd
+        def rotate(g, first, count):
             s = g % SEQ_GROUPS
-            tiles = slice(2 * half, 2 * half + 2)
-            table_shape = [P, 2, HEADS, ROT // 2]
+            tiles = slice(first, first + count)
+            table_shape = [P, count, HEADS, ROT // 2]
             cos_g = cos_sb[:, s, tiles, :].unsqueeze(2).to_broadcast(table_shape)
             sin_g = sin_sb[:, s, tiles, :].unsqueeze(2).to_broadcast(table_shape)
             neg_sin_g = neg_sin_sb[:, s, tiles, :].unsqueeze(2).to_broadcast(table_shape)
@@ -319,25 +329,28 @@ def tile_mla_pa_t_kernel(
             ].rearrange("p i h (j e) -> p i h j e", e=2)
             a = pairs[:, :, :, :, 0]
             b = pairs[:, :, :, :, 1]
-            by_cos = work.tile([P, 2, 2, HEADS, ROT // 2], F32)
-            by_sin = work.tile([P, 2, 2, HEADS, ROT // 2], F32)
-            engine.tensor_tensor(out=by_cos[:, 0], in0=a, in1=cos_g, op=ALU.mult)
-            engine.tensor_tensor(out=by_cos[:, 1], in0=b, in1=cos_g, op=ALU.mult)
-            engine.tensor_tensor(out=by_sin[:, 0], in0=b, in1=neg_sin_g, op=ALU.mult)
-            engine.tensor_tensor(out=by_sin[:, 1], in0=a, in1=sin_g, op=ALU.mult)
-            engine.tensor_tensor(
+            by_cos = rot.tile([P, 2, count, HEADS, ROT // 2], F32, tag="by_cos")
+            by_sin = rot.tile([P, 2, count, HEADS, ROT // 2], F32, tag="by_sin")
+            nc.gpsimd.tensor_tensor(out=by_cos[:, 0], in0=a, in1=cos_g, op=ALU.mult)
+            nc.gpsimd.tensor_tensor(out=by_cos[:, 1], in0=b, in1=cos_g, op=ALU.mult)
+            nc.gpsimd.tensor_tensor(out=by_sin[:, 0], in0=b, in1=neg_sin_g, op=ALU.mult)
+            nc.gpsimd.tensor_tensor(out=by_sin[:, 1], in0=a, in1=sin_g, op=ALU.mult)
+            nc.gpsimd.tensor_tensor(
                 out=pairs,
                 in0=by_cos[:].rearrange("p e i h j -> p i h j e"),
                 in1=by_sin[:].rearrange("p e i h j -> p i h j e"),
                 op=ALU.add,
             )
-
-        def store_k(g, half):
-            tiles = slice(2 * half, 2 * half + 2)
             nc.sync.dma_start(
                 out=k_rows[g * GROUP : (g + 1) * GROUP, :].rearrange("(p i) c -> p i c", i=TILES)[:, tiles, :],
                 in_=kv_out[g][:, tiles, 0, :],
             )
+
+        def rotate_and_store_k(g, half):
+            if g == GROUPS - 1:
+                rotate(g, 2 * half, 2)
+            elif half == 1:
+                rotate(g, 0, TILES)
 
         def store_v(g):
             nc.sync.dma_start(
@@ -351,23 +364,25 @@ def tile_mla_pa_t_kernel(
 
         def iteration(k):
             run(k + 4, load_x)
-            run(k + 2, transpose_x, 0)
             run(k + 1, quantise_x, 1)
             run(k + 1, project_kv, 2)
             run(k + 1, project_kv, 3)
+            run(k + 1, add_bias_and_sum, 0)
             run(k - 1, regroup_cn)
-            run(k - 1, quantise_cn)
-            for i in range(TILES):
+            for i in range(TILES - 1):
                 run(k, normalise, i)
             run(k, transpose_z, 0)
             run(k, transpose_z, 1)
-            run(k + 2, copy_x, 0)
-            for i in range(2):
-                run(k + 1, add_bias_and_sum, i)
-                run(k + 1, sum_squares, i)
-                run(k - 1, project_out, i)
+            run(k + 2, transpose_x, 0)
+            run(k + 1, sum_squares, 0)
+            run(k + 1, add_bias_and_sum, 1)
+            run(k + 1, sum_squares, 1)
+            run(k - 1, quantise_cn)
+            run(k - 1, project_out, 0)
+            run(k - 1, project_out, 1)
             run(k, gain_and_bias, 0)
             run(k, gain_and_bias, 1)
+            run(k + 2, copy_x, 0)
             run(k, transpose_z, 2)
             run(k + 2, transpose_x, 1)
             run(k + 1, add_bias_and_sum, 2)
@@ -384,17 +399,16 @@ def tile_mla_pa_t_kernel(
             run(k + 2, project_kv, 0)
             run(k - 1, add_out_bias, 1)
             run(k + 2, project_kv, 1)
-            run(k - 1, rotate, 0)
-            run(k - 1, store_k, 0)
+            run(k - 1, rotate_and_store_k, 0)
             run(k + 1, rstd_and_shift)
+            run(k + 1, normalise, TILES - 1)
             run(k, gain_and_bias, 2)
             run(k + 2, copy_x, 1)
             run(k, gain_and_bias, 3)
             run(k - 1, add_out_bias, 2)
             run(k - 1, add_out_bias, 3)
             run(k - 1, store_v)
-            run(k - 1, rotate, 1)
-            run(k - 1, store_k, 1)
+            run(k - 1, rotate_and_store_k, 1)
 
         iteration(-2)
         iteration(-1)

@@ -27,8 +27,8 @@ HEAD = K_COLS // HEADS
 ROT = 64
 TILES = 4
 GROUP = TILES * P
-GROUPS = TOKENS // GROUP
-SEQ_GROUPS = SEQ // GROUP
+BLOCKS = TOKENS // GROUP
+SEQ_BLOCKS = SEQ // GROUP
 EPS = 1e-5
 
 FLOPS = 2 * TOKENS * (DIM * KV_COLS + RANK * (NOPE_COLS + V_COLS))
@@ -49,6 +49,14 @@ def quantise(nc, codes, scales, grouped):
     )
 
 
+def token_groups():
+    groups = []
+    for block in range(BLOCKS):
+        tiles = TILES // 2 if block in (0, BLOCKS - 1) else TILES
+        groups.extend((block, first, tiles) for first in range(0, TILES, tiles))
+    return groups
+
+
 def tile_mla_pa_t_kernel(
     tc, x, wkv_a_w, wkv_a_b, kvn_g, kvn_b, wk_w, wk_b, wv_w, wv_b, cos, sin, out_0, out_1
 ):
@@ -56,16 +64,26 @@ def tile_mla_pa_t_kernel(
     x_rows = x.rearrange("b s d -> (b s) d")
     k_rows = out_0.rearrange("b s h e -> (b s) (h e)")
     v_rows = out_1.rearrange("b s h e -> (b s) (h e)")
+    groups = token_groups()
+
+    def rows_of(rows, g):
+        block, first, n = groups[g]
+        return rows[block * GROUP : (block + 1) * GROUP, :].rearrange("(p i) c -> p i c", i=TILES)[
+            :, first : first + n, :
+        ]
+
+    def tiles_of(g):
+        return groups[g][2]
 
     with ExitStack() as ctx:
         consts = ctx.enter_context(tc.tile_pool(name="consts", bufs=1))
         xin = ctx.enter_context(tc.tile_pool(name="xin", bufs=4))
         work = ctx.enter_context(tc.tile_pool(name="work", bufs=2))
         small = ctx.enter_context(tc.tile_pool(name="small", bufs=4))
-        outs = ctx.enter_context(tc.tile_pool(name="outs", bufs=4))
+        outs = ctx.enter_context(tc.tile_pool(name="outs", bufs=6))
         rot = ctx.enter_context(tc.tile_pool(name="rot", bufs=2))
-        psum_s = ctx.enter_context(tc.psum_pool(name="psum_s", bufs=3))
-        psum_v = ctx.enter_context(tc.psum_pool(name="psum_v", bufs=4))
+        psum_s = ctx.enter_context(tc.psum_pool(name="psum_s", bufs=4))
+        psum_v = ctx.enter_context(tc.psum_pool(name="psum_v", bufs=3))
         psum_r = ctx.enter_context(tc.psum_pool(name="psum_r", bufs=1))
         ctx.enter_context(tc.manual_schedule())
 
@@ -75,10 +93,7 @@ def tile_mla_pa_t_kernel(
 
         def load_x(g):
             x_tile = xin.tile([P, TILES, DIM], BF16)
-            nc.sync.dma_start(
-                out=x_tile[:],
-                in_=x_rows[g * GROUP : (g + 1) * GROUP, :].rearrange("(p i) d -> p i d", i=TILES),
-            )
+            nc.sync.dma_start(out=x_tile[:, 0 : tiles_of(g), :], in_=rows_of(x_rows, g))
             x_sb[g] = x_tile
 
         load_x(0)
@@ -104,12 +119,26 @@ def tile_mla_pa_t_kernel(
         b2_bc = consts.tile([P, 2, NOPE_COLS], BF16)
         nc.scalar.dma_start(out=b2_bc[:, 0, :], in_=wk_b.partition_broadcast(P))
         nc.scalar.dma_start(out=b2_bc[:, 1, :], in_=wv_b.partition_broadcast(P))
-        cos_sb = consts.tile([P, SEQ_GROUPS, TILES, ROT // 2], BF16)
+        cos_sb = consts.tile([P, SEQ_BLOCKS, TILES, ROT // 2], BF16)
         nc.scalar.dma_start(out=cos_sb[:], in_=cos.rearrange("(s p i) j -> p s i j", p=P, i=TILES))
-        sin_sb = consts.tile([P, SEQ_GROUPS, TILES, ROT // 2], BF16)
+        sin_sb = consts.tile([P, SEQ_BLOCKS, TILES, ROT // 2], BF16)
         nc.scalar.dma_start(out=sin_sb[:], in_=sin.rearrange("(s p i) j -> p s i j", p=P, i=TILES))
-        neg_sin_sb = consts.tile([P, SEQ_GROUPS, TILES, ROT // 2], BF16)
-        nc.gpsimd.tensor_scalar_mul(out=neg_sin_sb[:], in0=sin_sb[:], scalar1=-1.0)
+        cos_pairs = consts.tile([P, SEQ_BLOCKS * TILES, ROT // 2, 2], BF16)
+        sin_pairs = consts.tile([P, SEQ_BLOCKS * TILES, ROT // 2, 2], BF16)
+        for pairs, table, e, sign in (
+            (cos_pairs, cos_sb, 0, 1.0),
+            (cos_pairs, cos_sb, 1, 1.0),
+            (sin_pairs, sin_sb, 0, -1.0),
+            (sin_pairs, sin_sb, 1, 1.0),
+        ):
+            nc.gpsimd.tensor_scalar(
+                out=pairs[:, :, :, e],
+                in0=table[:].rearrange("p s i j -> p (s i) j"),
+                scalar1=sign,
+                scalar2=0.0,
+                op0=ALU.mult,
+                op1=ALU.add,
+            )
 
         warm = consts.tile([P, 1], F32)
         nc.scalar.activation(out=warm[:], in_=eps_col[:], func=ACT.Sqrt)
@@ -136,6 +165,8 @@ def tile_mla_pa_t_kernel(
             quantise(nc, w2_codes[:], w2_scales[:], w2_grouped[:])
 
         def transpose_x(g, half):
+            if 2 * half >= tiles_of(g):
+                return
             x_bank = psum_s.tile([P, 2, 2, P], F32, tag="to_scalar")
             x_t[g, half] = x_bank
             for i in range(2):
@@ -144,6 +175,8 @@ def tile_mla_pa_t_kernel(
                     nc.tensor.transpose(x_bank[:, i, u, :], x_words[:, u * P : (u + 1) * P], ident[:])
 
         def copy_x(g, half):
+            if 2 * half >= tiles_of(g):
+                return
             if half == 0:
                 grouped_tile = work.tile([P, GROUP * PACK], BF16, align_bytes=64)
                 x_grouped[g] = grouped_tile
@@ -154,40 +187,44 @@ def tile_mla_pa_t_kernel(
                 in_=x_t[g, half][:].rearrange("p i u w -> p i w u"),
             )
 
-        def quantise_x(g, half):
-            if half == 0:
-                codes_tile = work.tile([P, GROUP], U32, align_bytes=64)
-                scales_tile = work.tile([P, GROUP], U8, align_bytes=64)
-                x_codes[g], x_scales[g] = codes_tile, scales_tile
-            cols = slice(half * 2 * P, (half + 1) * 2 * P)
+        def quantise_x(g):
+            codes_tile = work.tile([P, GROUP], U32, align_bytes=64)
+            scales_tile = work.tile([P, GROUP], U8, align_bytes=64)
+            x_codes[g], x_scales[g] = codes_tile, scales_tile
+            cols = slice(0, tiles_of(g) * P)
             nc.vector.quantize_mx(
-                out=x_codes[g][:, cols].bitcast(FP8X4),
-                scales=x_scales[g][:, cols],
-                in_=x_grouped[g][:, half * 2 * P * PACK : (half + 1) * 2 * P * PACK],
+                out=codes_tile[:, cols].bitcast(FP8X4),
+                scales=scales_tile[:, cols],
+                in_=x_grouped[g][:, 0 : tiles_of(g) * P * PACK],
             )
 
-        def project_kv(g, i):
-            if i == 0:
-                rope_bank = psum_r.tile([P, TILES, ROPE_COLS], F32)
-                k_rope[g] = rope_bank
+        def project(g, i, out, cols):
             tokens = slice(i * P, (i + 1) * P)
-            latent_bank = psum_v.tile([P, RANK], F32, tag="to_vector")
-            latent[g, i] = latent_bank
-            for out, cols in (
-                (latent_bank[:], slice(ROPE_COLS, KV_COLS)),
-                (k_rope[g][:, i, :], slice(0, ROPE_COLS)),
-            ):
-                nc.tensor.matmul_mx(
-                    out=out,
-                    lhsT=x_codes[g][:, tokens].bitcast(FP8X4),
-                    lhsT_scale=x_scales[g][:, tokens],
-                    rhs=w1_codes[:, cols].bitcast(FP8X4),
-                    rhs_scale=w1_scales[:, cols],
-                    start=True,
-                    stop=True,
-                )
+            nc.tensor.matmul_mx(
+                out=out,
+                lhsT=x_codes[g][:, tokens].bitcast(FP8X4),
+                lhsT_scale=x_scales[g][:, tokens],
+                rhs=w1_codes[:, cols].bitcast(FP8X4),
+                rhs_scale=w1_scales[:, cols],
+                start=True,
+                stop=True,
+            )
+
+        def project_rope(g):
+            rope_bank = psum_r.tile([P, TILES, ROPE_COLS], F32)
+            k_rope[g] = rope_bank
+            for i in range(tiles_of(g)):
+                project(g, i, rope_bank[:, i, :], slice(0, ROPE_COLS))
+
+        def project_latent(g, i):
+            if i < tiles_of(g):
+                latent_bank = psum_v.tile([P, RANK], F32, tag="to_vector")
+                latent[g, i] = latent_bank
+                project(g, i, latent_bank[:], slice(ROPE_COLS, KV_COLS))
 
         def add_bias_and_sum(g, i):
+            if i >= tiles_of(g):
+                return
             if i == 0:
                 c_tile = work.tile([P, TILES, RANK], F32)
                 sums_tile = small.tile([P, TILES], F32)
@@ -203,6 +240,8 @@ def tile_mla_pa_t_kernel(
             )
 
         def sum_squares(g, i):
+            if i >= tiles_of(g):
+                return
             if i == 0:
                 sum_sq_tile = small.tile([P, TILES], F32)
                 sum_sq[g] = sum_sq_tile
@@ -219,20 +258,22 @@ def tile_mla_pa_t_kernel(
         def std_dev(g):
             std_tile = small.tile([P, TILES], F32)
             std[g] = std_tile
+            n = tiles_of(g)
             nc.scalar.activation(
-                out=std_tile[:], in_=sum_sq[g][:], func=ACT.Sqrt, bias=eps_col[:], scale=1.0 / RANK**3
+                out=std_tile[:, 0:n], in_=sum_sq[g][:, 0:n], func=ACT.Sqrt, bias=eps_col[:], scale=1.0 / RANK**3
             )
 
         def rstd_and_shift(g):
             rstd_tile = small.tile([P, TILES], F32)
             shift_tile = small.tile([P, TILES], F32)
             rstd[g], shift[g] = rstd_tile, shift_tile
-            nc.vector.reciprocal(out=rstd_tile[:], in_=std[g][:])
+            n = tiles_of(g)
+            nc.vector.reciprocal(out=rstd_tile[:, 0:n], in_=std[g][:, 0:n])
             nc.vector.scalar_tensor_tensor(
-                out=shift_tile[:],
-                in0=sums[g][:],
+                out=shift_tile[:, 0:n],
+                in0=sums[g][:, 0:n],
                 scalar=-1.0 / RANK,
-                in1=rstd_tile[:],
+                in1=rstd_tile[:, 0:n],
                 op0=ALU.mult,
                 op1=ALU.mult,
             )
@@ -240,15 +281,18 @@ def tile_mla_pa_t_kernel(
         def add_rope_bias(g):
             kv_tile = outs.tile([P, TILES, 2, K_COLS], F32)
             kv_out[g] = kv_tile
+            n = tiles_of(g)
             nc.vector.tensor_tensor(
-                out=kv_tile[:, :, 0, NOPE_COLS:K_COLS],
-                in0=k_rope[g][:],
-                in1=b1_bc[:, 0:ROPE_COLS].unsqueeze(1).to_broadcast([P, TILES, ROPE_COLS]),
+                out=kv_tile[:, 0:n, 0, NOPE_COLS:K_COLS],
+                in0=k_rope[g][:, 0:n, :],
+                in1=b1_bc[:, 0:ROPE_COLS].unsqueeze(1).to_broadcast([P, n, ROPE_COLS]),
                 op=ALU.add,
             )
 
         def normalise(g, i):
-            if g not in z:
+            if i >= tiles_of(g):
+                return
+            if i == 0:
                 z_tile = work.tile([P, TILES, RANK], F32)
                 z[g] = z_tile
             if i == TILES - 1:
@@ -272,16 +316,17 @@ def tile_mla_pa_t_kernel(
         def transpose_z(g, t):
             z_bank = psum_s.tile([P, TILES, P], F32, tag="to_scalar")
             z_t[g, t] = z_bank
-            for i in range(TILES):
+            for i in range(tiles_of(g)):
                 nc.tensor.transpose(z_bank[:, i, :], z[g][:, i, t * P : (t + 1) * P], ident[:])
 
         def gain_and_bias(g, t):
             if t == 0:
                 planes_tile = work.tile([P, PACK, GROUP], BF16)
                 cn_planes[g] = planes_tile
+            n = tiles_of(g)
             nc.scalar.activation(
-                out=cn_planes[g][:, t, :],
-                in_=z_t[g, t][:].rearrange("p i w -> p (i w)"),
+                out=cn_planes[g][:, t, 0 : n * P],
+                in_=z_t[g, t][:, 0:n, :].rearrange("p i w -> p (i w)"),
                 func=ACT.Identity,
                 bias=gb_col[:, PACK + t : PACK + t + 1],
                 scale=gb_col[:, t : t + 1],
@@ -290,15 +335,19 @@ def tile_mla_pa_t_kernel(
         def regroup_cn(g):
             cn_grouped_tile = work.tile([P, GROUP, PACK], BF16, align_bytes=64)
             cn_grouped[g] = cn_grouped_tile
-            regroup(nc, cn_grouped_tile[:], cn_planes[g][:])
+            cols = slice(0, tiles_of(g) * P)
+            regroup(nc, cn_grouped_tile[:, cols, :], cn_planes[g][:, :, cols])
 
         def quantise_cn(g):
             cn_codes_tile = work.tile([P, GROUP], U32, align_bytes=64)
             cn_scales_tile = work.tile([P, GROUP], U8, align_bytes=64)
             cn_codes[g], cn_scales[g] = cn_codes_tile, cn_scales_tile
-            quantise(nc, cn_codes_tile[:], cn_scales_tile[:], cn_grouped[g][:])
+            cols = slice(0, tiles_of(g) * P)
+            quantise(nc, cn_codes_tile[:, cols], cn_scales_tile[:, cols], cn_grouped[g][:, cols, :])
 
         def project_out(g, i):
+            if i >= tiles_of(g):
+                return
             tokens = slice(i * P, (i + 1) * P)
             out_bank = psum_v.tile([P, 2, NOPE_COLS], F32, tag="to_vector")
             nope_v[g, i] = out_bank
@@ -313,105 +362,89 @@ def tile_mla_pa_t_kernel(
             )
 
         def add_out_bias(g, i):
-            nc.vector.tensor_tensor(
-                out=kv_out[g][:, i, :, 0:NOPE_COLS], in0=nope_v[g, i][:], in1=b2_bc[:], op=ALU.add
-            )
+            if i < tiles_of(g):
+                nc.vector.tensor_tensor(
+                    out=kv_out[g][:, i, :, 0:NOPE_COLS], in0=nope_v[g, i][:], in1=b2_bc[:], op=ALU.add
+                )
 
-        def rotate(g, first, count):
-            s = g % SEQ_GROUPS
-            tiles = slice(first, first + count)
-            table_shape = [P, count, HEADS, ROT // 2]
-            cos_g = cos_sb[:, s, tiles, :].unsqueeze(2).to_broadcast(table_shape)
-            sin_g = sin_sb[:, s, tiles, :].unsqueeze(2).to_broadcast(table_shape)
-            neg_sin_g = neg_sin_sb[:, s, tiles, :].unsqueeze(2).to_broadcast(table_shape)
-            pairs = kv_out[g][:, tiles, 0, :].rearrange("p i (h e) -> p i h e", h=HEADS)[
-                :, :, :, HEAD - ROT : HEAD
-            ].rearrange("p i h (j e) -> p i h j e", e=2)
-            a = pairs[:, :, :, :, 0]
-            b = pairs[:, :, :, :, 1]
-            by_cos = rot.tile([P, 2, count, HEADS, ROT // 2], F32, tag="by_cos")
-            by_sin = rot.tile([P, 2, count, HEADS, ROT // 2], F32, tag="by_sin")
-            nc.gpsimd.tensor_tensor(out=by_cos[:, 0], in0=a, in1=cos_g, op=ALU.mult)
-            nc.gpsimd.tensor_tensor(out=by_cos[:, 1], in0=b, in1=cos_g, op=ALU.mult)
-            nc.gpsimd.tensor_tensor(out=by_sin[:, 0], in0=b, in1=neg_sin_g, op=ALU.mult)
-            nc.gpsimd.tensor_tensor(out=by_sin[:, 1], in0=a, in1=sin_g, op=ALU.mult)
-            nc.gpsimd.tensor_tensor(
-                out=pairs,
-                in0=by_cos[:].rearrange("p e i h j -> p i h j e"),
-                in1=by_sin[:].rearrange("p e i h j -> p i h j e"),
-                op=ALU.add,
-            )
-            nc.sync.dma_start(
-                out=k_rows[g * GROUP : (g + 1) * GROUP, :].rearrange("(p i) c -> p i c", i=TILES)[:, tiles, :],
-                in_=kv_out[g][:, tiles, 0, :],
-            )
+        def rotate(g, head):
+            block, first, n = groups[g]
+            position = block % SEQ_BLOCKS * TILES + first
+            cos_g = cos_pairs[:, position : position + n, :, :]
+            sin_g = sin_pairs[:, position : position + n, :, :]
+            end = (head + 1) * HEAD
+            pairs = kv_out[g][:, 0:n, 0, end - ROT : end].rearrange("p i (j e) -> p i j e", e=2)
+            by_cos = rot.tile([P, n, ROT // 2, 2], F32, tag="by_cos")
+            by_sin = rot.tile([P, n, ROT // 2, 2], F32, tag="by_sin")
+            nc.gpsimd.tensor_tensor(out=by_cos[:], in0=pairs, in1=cos_g, op=ALU.mult)
+            nc.gpsimd.tensor_tensor(out=by_sin[:], in0=pairs[:, :, :, ::-1], in1=sin_g, op=ALU.mult)
+            nc.gpsimd.tensor_tensor(out=pairs, in0=by_cos[:], in1=by_sin[:], op=ALU.add)
 
-        def rotate_and_store_k(g, half):
-            if g == GROUPS - 1:
-                rotate(g, 2 * half, 2)
-            elif half == 1:
-                rotate(g, 0, TILES)
+        def store_k(g):
+            n = tiles_of(g)
+            nc.sync.dma_start(out=rows_of(k_rows, g), in_=kv_out[g][:, 0:n, 0, :])
 
         def store_v(g):
-            nc.sync.dma_start(
-                out=v_rows[g * GROUP : (g + 1) * GROUP, :].rearrange("(p i) c -> p i c", i=TILES),
-                in_=kv_out[g][:, :, 1, 0:V_COLS],
-            )
+            n = tiles_of(g)
+            nc.sync.dma_start(out=rows_of(v_rows, g), in_=kv_out[g][:, 0:n, 1, 0:V_COLS])
 
         def run(g, step, *args):
-            if 0 <= g < GROUPS:
+            if 0 <= g < len(groups):
                 step(g, *args)
 
         def iteration(k):
             run(k + 4, load_x)
-            run(k + 1, quantise_x, 1)
-            run(k + 1, project_kv, 2)
-            run(k + 1, project_kv, 3)
-            run(k + 1, add_bias_and_sum, 0)
-            run(k - 1, regroup_cn)
-            for i in range(TILES - 1):
-                run(k, normalise, i)
-            run(k, transpose_z, 0)
-            run(k, transpose_z, 1)
+            run(k, quantise_x)
+            run(k + 1, copy_x, 0)
+            run(k + 1, copy_x, 1)
+            run(k - 2, transpose_z, 0)
+            run(k - 2, transpose_z, 1)
+            run(k - 2, transpose_z, 2)
+            run(k - 2, transpose_z, 3)
+            run(k - 3, regroup_cn)
+            run(k - 1, rstd_and_shift)
+            run(k - 2, gain_and_bias, 0)
+            run(k - 2, gain_and_bias, 1)
+            run(k, project_rope)
+            run(k, project_latent, 0)
+            run(k, project_latent, 1)
+            run(k, project_latent, 2)
+            run(k - 3, quantise_cn)
+            run(k, add_rope_bias)
+            run(k, rotate, 1)
+            run(k - 4, rotate, 0)
+            run(k - 4, store_k)
+            run(k - 1, normalise, 0)
+            run(k - 1, normalise, 1)
+            run(k - 1, normalise, 3)
+            run(k - 2, gain_and_bias, 2)
+            run(k - 2, gain_and_bias, 3)
             run(k + 2, transpose_x, 0)
-            run(k + 1, sum_squares, 0)
-            run(k + 1, add_bias_and_sum, 1)
-            run(k + 1, sum_squares, 1)
-            run(k - 1, quantise_cn)
-            run(k - 1, project_out, 0)
-            run(k - 1, project_out, 1)
-            run(k, gain_and_bias, 0)
-            run(k, gain_and_bias, 1)
-            run(k + 2, copy_x, 0)
-            run(k, transpose_z, 2)
             run(k + 2, transpose_x, 1)
-            run(k + 1, add_bias_and_sum, 2)
-            run(k + 1, sum_squares, 2)
-            run(k - 1, project_out, 2)
-            run(k, transpose_z, 3)
-            run(k + 1, add_bias_and_sum, 3)
-            run(k + 1, sum_squares, 3)
-            run(k - 1, project_out, 3)
-            run(k + 1, std_dev)
-            run(k + 1, add_rope_bias)
-            run(k - 1, add_out_bias, 0)
-            run(k + 2, quantise_x, 0)
-            run(k + 2, project_kv, 0)
-            run(k - 1, add_out_bias, 1)
-            run(k + 2, project_kv, 1)
-            run(k - 1, rotate_and_store_k, 0)
-            run(k + 1, rstd_and_shift)
-            run(k + 1, normalise, TILES - 1)
-            run(k, gain_and_bias, 2)
-            run(k + 2, copy_x, 1)
-            run(k, gain_and_bias, 3)
-            run(k - 1, add_out_bias, 2)
-            run(k - 1, add_out_bias, 3)
-            run(k - 1, store_v)
-            run(k - 1, rotate_and_store_k, 1)
+            run(k - 1, normalise, 2)
+            run(k, add_bias_and_sum, 0)
+            run(k, project_latent, 3)
+            run(k, sum_squares, 0)
+            run(k, add_bias_and_sum, 1)
+            run(k, sum_squares, 1)
+            run(k - 3, project_out, 0)
+            run(k, add_bias_and_sum, 2)
+            run(k - 3, project_out, 1)
+            run(k, sum_squares, 2)
+            run(k, add_bias_and_sum, 3)
+            run(k, sum_squares, 3)
+            run(k, std_dev)
+            run(k - 3, project_out, 2)
+            run(k - 3, add_out_bias, 0)
+            run(k - 3, project_out, 3)
+            run(k - 3, add_out_bias, 1)
+            run(k - 3, add_out_bias, 2)
+            run(k - 3, add_out_bias, 3)
+            run(k - 3, store_v)
 
         iteration(-2)
         iteration(-1)
+        iteration(0)
         prepare_second_stage()
-        for k in range(GROUPS + 1):
+        for k in range(1, len(groups) + 4):
             iteration(k)

@@ -88,7 +88,7 @@ def tile_mla_pa_t_kernel(
         ctx.enter_context(tc.manual_schedule())
 
         x_sb, x_t, x_grouped, x_codes, x_scales = {}, {}, {}, {}, {}
-        latent, k_rope, c, sums, sum_sq, std, rstd, shift, z, z_t = {}, {}, {}, {}, {}, {}, {}, {}, {}, {}
+        latent, k_rope, c, sums, sum_sq, neg_mean, rstd, shift, z, z_t = {}, {}, {}, {}, {}, {}, {}, {}, {}, {}
         cn_planes, cn_grouped, cn_codes, cn_scales, nope_v, kv_out = {}, {}, {}, {}, {}, {}
 
         def load_x(g):
@@ -96,73 +96,88 @@ def tile_mla_pa_t_kernel(
             nc.sync.dma_start(out=x_tile[:, 0 : tiles_of(g), :], in_=rows_of(x_rows, g))
             x_sb[g] = x_tile
 
-        load_x(0)
+        bias_rows = consts.tile([P, KV_COLS + NOPE_COLS + V_COLS], BF16)
+        nc.vector.memset(bias_rows[:], 0.0)
+        gb_rows = consts.tile([P, P], BF16)
+        nc.vector.memset(gb_rows[:], 0.0)
+        eps_col = consts.tile([P, 1], F32)
+        nc.vector.memset(eps_col[:], EPS)
+        ones = consts.tile([P, P], BF16)
+        nc.vector.memset(ones[:], 1.0)
+        ident = consts.tile([P, P], F32)
+        make_identity(nc, ident[:])
+
         w1_raw = consts.tile([P, 2, 2, KV_COLS], BF16)
-        nc.sync.dma_start(out=w1_raw[:], in_=wkv_a_w.rearrange("(u q e) c -> q u e c", u=2, e=2))
+        w1_rows = wkv_a_w.rearrange("(u q e) c -> q u e c", u=2, e=2)
+        w1_parts = (slice(0, KV_COLS // 2), slice(KV_COLS // 2, KV_COLS))
+        for cols in w1_parts:
+            for u in range(2):
+                nc.sync.dma_start(out=w1_raw[:, u, :, cols], in_=w1_rows[:, u, :, cols])
+        load_x(0)
+
+        row = 0
+        for bias in (wkv_a_b, wk_b, wv_b):
+            n = bias.shape[0]
+            nc.sync.dma_start(out=bias_rows[0:1, row : row + n], in_=bias.rearrange("(o n) -> o n", o=1))
+            row += n
+        nc.sync.dma_start(out=gb_rows[0:PACK, :], in_=kvn_g.rearrange("(t p) -> t p", p=P))
+        nc.sync.dma_start(out=gb_rows[PACK : 2 * PACK, :], in_=kvn_b.rearrange("(t p) -> t p", p=P))
+        warm = consts.tile([P, 1], F32)
+        nc.scalar.activation(out=warm[:], in_=eps_col[:], func=ACT.Abs_reciprocal_sqrt)
+
         load_x(1)
+        cos_sb = consts.tile([P, SEQ_BLOCKS, TILES, ROT // 2], BF16)
+        nc.sync.dma_start(out=cos_sb[:], in_=cos.rearrange("(s p i) j -> p s i j", p=P, i=TILES))
+        sin_sb = consts.tile([P, SEQ_BLOCKS, TILES, ROT // 2], BF16)
+        nc.sync.dma_start(out=sin_sb[:], in_=sin.rearrange("(s p i) j -> p s i j", p=P, i=TILES))
         w2_raw = consts.tile([P, PACK, NOPE_COLS + V_COLS], BF16)
         nc.sync.dma_start(out=w2_raw[:, :, 0:NOPE_COLS], in_=wk_w.rearrange("(t p) n -> p t n", p=P))
         nc.sync.dma_start(out=w2_raw[:, :, NOPE_COLS:], in_=wv_w.rearrange("(t p) n -> p t n", p=P))
 
-        ident = consts.tile([P, P], F32)
-        make_identity(nc, ident[:])
-
-        eps_col = consts.tile([P, 1], F32)
-        nc.vector.memset(eps_col[:], EPS)
-        gb_rows = consts.tile([P, P], BF16)
-        nc.vector.memset(gb_rows[:], 0.0)
-
         b1_bc = consts.tile([P, KV_COLS], BF16)
-        nc.scalar.dma_start(out=b1_bc[:], in_=wkv_a_b.partition_broadcast(P))
-        nc.scalar.dma_start(out=gb_rows[0:PACK, :], in_=kvn_g.rearrange("(t p) -> t p", p=P))
-        nc.scalar.dma_start(out=gb_rows[PACK : 2 * PACK, :], in_=kvn_b.rearrange("(t p) -> t p", p=P))
         b2_bc = consts.tile([P, 2, NOPE_COLS], BF16)
-        nc.scalar.dma_start(out=b2_bc[:, 0, :], in_=wk_b.partition_broadcast(P))
-        nc.scalar.dma_start(out=b2_bc[:, 1, :], in_=wv_b.partition_broadcast(P))
-        cos_sb = consts.tile([P, SEQ_BLOCKS, TILES, ROT // 2], BF16)
-        nc.scalar.dma_start(out=cos_sb[:], in_=cos.rearrange("(s p i) j -> p s i j", p=P, i=TILES))
-        sin_sb = consts.tile([P, SEQ_BLOCKS, TILES, ROT // 2], BF16)
-        nc.scalar.dma_start(out=sin_sb[:], in_=sin.rearrange("(s p i) j -> p s i j", p=P, i=TILES))
-        cos_pairs = consts.tile([P, SEQ_BLOCKS * TILES, ROT // 2, 2], BF16)
-        sin_pairs = consts.tile([P, SEQ_BLOCKS * TILES, ROT // 2, 2], BF16)
-        for pairs, table, e, sign in (
-            (cos_pairs, cos_sb, 0, 1.0),
-            (cos_pairs, cos_sb, 1, 1.0),
-            (sin_pairs, sin_sb, 0, -1.0),
-            (sin_pairs, sin_sb, 1, 1.0),
-        ):
-            nc.gpsimd.tensor_scalar(
-                out=pairs[:, :, :, e],
-                in0=table[:].rearrange("p s i j -> p (s i) j"),
-                scalar1=sign,
-                scalar2=0.0,
-                op0=ALU.mult,
-                op1=ALU.add,
-            )
 
-        warm = consts.tile([P, 1], F32)
-        nc.scalar.activation(out=warm[:], in_=eps_col[:], func=ACT.Sqrt)
+        def repeat_biases():
+            for out, first in (
+                (b1_bc[:, 0:ROPE_COLS], 0),
+                (b1_bc[:, ROPE_COLS:KV_COLS], ROPE_COLS),
+                (b2_bc[:].rearrange("p s c -> p (s c)"), KV_COLS),
+            ):
+                n = out.shape[1]
+                bias_bank = psum_v.tile([P, RANK], F32, tag="to_vector")
+                nc.tensor.matmul(
+                    out=bias_bank[:, 0:n], lhsT=ones[:], rhs=bias_rows[:, first : first + n], start=True, stop=True
+                )
+                nc.scalar.copy(out=out, in_=bias_bank[:, 0:n])
+
+        gb_f32 = consts.tile([P, P], F32)
+        gb_col = consts.tile([P, 2 * PACK], F32)
+
+        def spread_gain_and_bias():
+            gb_t = psum_s.tile([P, TILES, P], F32, tag="to_scalar")
+            nc.tensor.transpose(gb_t[:, 0, :], gb_f32[:], ident[:])
+            nc.vector.tensor_copy(out=gb_col[:], in_=gb_t[:, 0, 0 : 2 * PACK])
+
+        cos_pairs = consts.tile([P, SEQ_BLOCKS * TILES, ROT // 2, 2], BF16)
+        neg_sin_sb = consts.tile([P, SEQ_BLOCKS, TILES, ROT // 2], BF16)
+        for out, table, sign in (
+            (cos_pairs[:, :, :, 0], cos_sb[:].rearrange("p s i j -> p (s i) j"), 1.0),
+            (cos_pairs[:, :, :, 1], cos_sb[:].rearrange("p s i j -> p (s i) j"), 1.0),
+            (neg_sin_sb[:], sin_sb[:], -1.0),
+        ):
+            nc.gpsimd.tensor_scalar(out=out, in0=table, scalar1=sign, scalar2=0.0, op0=ALU.mult, op1=ALU.add)
 
         w1_grouped = consts.tile([P, KV_COLS, PACK], BF16, align_bytes=64)
         w1_codes = consts.tile([P, KV_COLS], U32, align_bytes=64)
         w1_scales = consts.tile([P, KV_COLS], U8, align_bytes=64)
-        regroup(nc, w1_grouped[:], w1_raw[:].rearrange("p u e c -> p (u e) c"))
+        for cols in w1_parts:
+            regroup(nc, w1_grouped[:, cols, :], w1_raw[:, :, :, cols].rearrange("p u e c -> p (u e) c"))
         for cols in (slice(0, ROPE_COLS), slice(ROPE_COLS, KV_COLS)):
             quantise(nc, w1_codes[:, cols], w1_scales[:, cols], w1_grouped[:, cols, :])
 
         w2_grouped = consts.tile([P, NOPE_COLS + V_COLS, PACK], BF16, align_bytes=64)
         w2_codes = consts.tile([P, NOPE_COLS + V_COLS], U32, align_bytes=64)
         w2_scales = consts.tile([P, NOPE_COLS + V_COLS], U8, align_bytes=64)
-        gb_col = consts.tile([P, 2 * PACK], F32)
-
-        def prepare_second_stage():
-            gb_f32 = consts.tile([P, P], F32)
-            nc.vector.tensor_copy(out=gb_f32[:], in_=gb_rows[:])
-            gb_t = psum_s.tile([P, TILES, P], F32, tag="to_scalar")
-            nc.tensor.transpose(gb_t[:, 0, :], gb_f32[:], ident[:])
-            regroup(nc, w2_grouped[:], w2_raw[:])
-            nc.vector.tensor_copy(out=gb_col[:], in_=gb_t[:, 0, 0 : 2 * PACK])
-            quantise(nc, w2_codes[:], w2_scales[:], w2_grouped[:])
 
         def transpose_x(g, half):
             if 2 * half >= tiles_of(g):
@@ -255,62 +270,66 @@ def tile_mla_pa_t_kernel(
                 accum_out=sum_sq[g][:, i : i + 1],
             )
 
-        def std_dev(g):
-            std_tile = small.tile([P, TILES], F32)
-            std[g] = std_tile
+        def inverse_deviation(g):
             n = tiles_of(g)
+            neg_mean_tile = small.tile([P, TILES], F32)
+            rstd_tile = small.tile([P, TILES], F32)
+            neg_mean[g], rstd[g] = neg_mean_tile, rstd_tile
+            nc.scalar.mul(neg_mean_tile[:, 0:n], sums[g][:, 0:n], -1.0 / RANK)
             nc.scalar.activation(
-                out=std_tile[:, 0:n], in_=sum_sq[g][:, 0:n], func=ACT.Sqrt, bias=eps_col[:], scale=1.0 / RANK**3
+                out=rstd_tile[:, 0:n],
+                in_=sum_sq[g][:, 0:n],
+                func=ACT.Abs_reciprocal_sqrt,
+                bias=eps_col[:],
+                scale=1.0 / RANK**3,
             )
 
-        def rstd_and_shift(g):
-            rstd_tile = small.tile([P, TILES], F32)
+        def shifts(g):
             shift_tile = small.tile([P, TILES], F32)
-            rstd[g], shift[g] = rstd_tile, shift_tile
-            n = tiles_of(g)
-            nc.vector.reciprocal(out=rstd_tile[:, 0:n], in_=std[g][:, 0:n])
-            nc.vector.scalar_tensor_tensor(
-                out=shift_tile[:, 0:n],
-                in0=sums[g][:, 0:n],
-                scalar=-1.0 / RANK,
-                in1=rstd_tile[:, 0:n],
-                op0=ALU.mult,
-                op1=ALU.mult,
-            )
+            shift[g] = shift_tile
+            for i in range(tiles_of(g)):
+                nc.scalar.activation(
+                    out=shift_tile[:, i : i + 1],
+                    in_=neg_mean[g][:, i : i + 1],
+                    func=ACT.Copy,
+                    scale=rstd[g][:, i : i + 1],
+                )
 
         def add_rope_bias(g):
-            kv_tile = outs.tile([P, TILES, 2, K_COLS], F32)
+            kv_tile = outs.tile([P, 2, TILES, K_COLS], F32)
             kv_out[g] = kv_tile
             n = tiles_of(g)
             nc.vector.tensor_tensor(
-                out=kv_tile[:, 0:n, 0, NOPE_COLS:K_COLS],
+                out=kv_tile[:, 0, 0:n, NOPE_COLS:K_COLS],
                 in0=k_rope[g][:, 0:n, :],
                 in1=b1_bc[:, 0:ROPE_COLS].unsqueeze(1).to_broadcast([P, n, ROPE_COLS]),
                 op=ALU.add,
             )
 
-        def normalise(g, i):
+        def normalise(g, i, engine=None):
             if i >= tiles_of(g):
                 return
             if i == 0:
                 z_tile = work.tile([P, TILES, RANK], F32)
                 z[g] = z_tile
-            if i == TILES - 1:
-                nc.gpsimd.tensor_scalar(
-                    out=z[g][:, i, :],
-                    in0=c[g][:, i, :],
-                    scalar1=rstd[g][:, i : i + 1],
-                    scalar2=shift[g][:, i : i + 1],
-                    op0=ALU.mult,
-                    op1=ALU.add,
-                )
-            else:
+            if engine is None and i >= TILES // 2:
+                engine = nc.gpsimd
+            if engine is None:
                 nc.scalar.activation(
                     out=z[g][:, i, :],
                     in_=c[g][:, i, :],
                     func=ACT.Identity,
                     bias=shift[g][:, i : i + 1],
                     scale=rstd[g][:, i : i + 1],
+                )
+            else:
+                engine.tensor_scalar(
+                    out=z[g][:, i, :],
+                    in0=c[g][:, i, :],
+                    scalar1=rstd[g][:, i : i + 1],
+                    scalar2=shift[g][:, i : i + 1],
+                    op0=ALU.mult,
+                    op1=ALU.add,
                 )
 
         def transpose_z(g, t):
@@ -364,29 +383,42 @@ def tile_mla_pa_t_kernel(
         def add_out_bias(g, i):
             if i < tiles_of(g):
                 nc.vector.tensor_tensor(
-                    out=kv_out[g][:, i, :, 0:NOPE_COLS], in0=nope_v[g, i][:], in1=b2_bc[:], op=ALU.add
+                    out=kv_out[g][:, :, i, 0:NOPE_COLS], in0=nope_v[g, i][:], in1=b2_bc[:], op=ALU.add
                 )
 
-        def rotate(g, head):
+        def rotate(g, engine=nc.gpsimd):
             block, first, n = groups[g]
-            position = block % SEQ_BLOCKS * TILES + first
-            cos_g = cos_pairs[:, position : position + n, :, :]
-            sin_g = sin_pairs[:, position : position + n, :, :]
-            end = (head + 1) * HEAD
-            pairs = kv_out[g][:, 0:n, 0, end - ROT : end].rearrange("p i (j e) -> p i j e", e=2)
-            by_cos = rot.tile([P, n, ROT // 2, 2], F32, tag="by_cos")
-            by_sin = rot.tile([P, n, ROT // 2, 2], F32, tag="by_sin")
-            nc.gpsimd.tensor_tensor(out=by_cos[:], in0=pairs, in1=cos_g, op=ALU.mult)
-            nc.gpsimd.tensor_tensor(out=by_sin[:], in0=pairs[:, :, :, ::-1], in1=sin_g, op=ALU.mult)
-            nc.gpsimd.tensor_tensor(out=pairs, in0=by_cos[:], in1=by_sin[:], op=ALU.add)
+            s = block % SEQ_BLOCKS
+            positions = slice(first, first + n)
+            cos_g = cos_pairs[:, s * TILES + first : s * TILES + first + n, :, :].rearrange("p i j e -> p i (j e)")
+            rotated = kv_out[g][:, 0, 0:n, :].rearrange("p i (h e) -> p i h e", h=HEADS)[:, :, :, HEAD - ROT : HEAD]
+            pairs = rotated.rearrange("p i h (j e) -> p i h j e", e=2)
+            by_cos = rot.tile([P, n, HEADS, ROT], F32, tag="by_cos")
+            by_sin = rot.tile([P, 2, n, HEADS, ROT // 2], F32, tag="by_sin")
+            engine.tensor_tensor(
+                out=by_cos[:], in0=rotated, in1=cos_g.unsqueeze(2).to_broadcast([P, n, HEADS, ROT]), op=ALU.mult
+            )
+            for e, table in ((0, neg_sin_sb), (1, sin_sb)):
+                engine.tensor_tensor(
+                    out=by_sin[:, e],
+                    in0=pairs[:, :, :, :, 1 - e],
+                    in1=table[:, s, positions, :].unsqueeze(2).to_broadcast([P, n, HEADS, ROT // 2]),
+                    op=ALU.mult,
+                )
+            engine.tensor_tensor(
+                out=pairs,
+                in0=by_cos[:].rearrange("p i h (j e) -> p i h j e", e=2),
+                in1=by_sin[:].rearrange("p e i h j -> p i h j e"),
+                op=ALU.add,
+            )
 
         def store_k(g):
             n = tiles_of(g)
-            nc.sync.dma_start(out=rows_of(k_rows, g), in_=kv_out[g][:, 0:n, 0, :])
+            nc.sync.dma_start(out=rows_of(k_rows, g), in_=kv_out[g][:, 0, 0:n, :])
 
         def store_v(g):
             n = tiles_of(g)
-            nc.sync.dma_start(out=rows_of(v_rows, g), in_=kv_out[g][:, 0:n, 1, 0:V_COLS])
+            nc.sync.dma_start(out=rows_of(v_rows, g), in_=kv_out[g][:, 1, 0:n, 0:V_COLS])
 
         def run(g, step, *args):
             if 0 <= g < len(groups):
@@ -394,57 +426,92 @@ def tile_mla_pa_t_kernel(
 
         def iteration(k):
             run(k + 4, load_x)
-            run(k, quantise_x)
             run(k + 1, copy_x, 0)
             run(k + 1, copy_x, 1)
-            run(k - 2, transpose_z, 0)
-            run(k - 2, transpose_z, 1)
-            run(k - 2, transpose_z, 2)
-            run(k - 2, transpose_z, 3)
-            run(k - 3, regroup_cn)
-            run(k - 1, rstd_and_shift)
-            run(k - 2, gain_and_bias, 0)
-            run(k - 2, gain_and_bias, 1)
-            run(k, project_rope)
-            run(k, project_latent, 0)
-            run(k, project_latent, 1)
-            run(k, project_latent, 2)
-            run(k - 3, quantise_cn)
-            run(k, add_rope_bias)
-            run(k, rotate, 1)
-            run(k - 4, rotate, 0)
-            run(k - 4, store_k)
             run(k - 1, normalise, 0)
             run(k - 1, normalise, 1)
-            run(k - 1, normalise, 3)
-            run(k - 2, gain_and_bias, 2)
-            run(k - 2, gain_and_bias, 3)
-            run(k + 2, transpose_x, 0)
-            run(k + 2, transpose_x, 1)
             run(k - 1, normalise, 2)
+            run(k - 1, normalise, 3)
+            run(k, add_rope_bias)
             run(k, add_bias_and_sum, 0)
             run(k, project_latent, 3)
             run(k, sum_squares, 0)
             run(k, add_bias_and_sum, 1)
             run(k, sum_squares, 1)
-            run(k - 3, project_out, 0)
+            run(k - 3, rotate)
+            run(k - 3, store_k)
+            run(k - 1, transpose_z, 0)
+            run(k - 1, transpose_z, 1)
+            run(k - 1, transpose_z, 2)
+            run(k - 1, transpose_z, 3)
+            run(k - 2, regroup_cn)
+            run(k - 1, gain_and_bias, 0)
+            run(k + 2, transpose_x, 0)
             run(k, add_bias_and_sum, 2)
-            run(k - 3, project_out, 1)
             run(k, sum_squares, 2)
+            run(k - 2, quantise_cn)
+            run(k - 1, gain_and_bias, 1)
+            run(k - 2, project_out, 0)
+            run(k - 2, project_out, 1)
             run(k, add_bias_and_sum, 3)
             run(k, sum_squares, 3)
-            run(k, std_dev)
-            run(k - 3, project_out, 2)
-            run(k - 3, add_out_bias, 0)
-            run(k - 3, project_out, 3)
-            run(k - 3, add_out_bias, 1)
-            run(k - 3, add_out_bias, 2)
-            run(k - 3, add_out_bias, 3)
-            run(k - 3, store_v)
+            run(k, inverse_deviation)
+            run(k - 2, project_out, 2)
+            run(k - 1, gain_and_bias, 2)
+            run(k, shifts)
+            run(k - 1, gain_and_bias, 3)
+            run(k + 1, quantise_x)
+            run(k - 2, add_out_bias, 0)
+            run(k - 2, project_out, 3)
+            run(k + 2, transpose_x, 1)
+            run(k + 1, project_rope)
+            run(k - 2, add_out_bias, 1)
+            run(k + 1, project_latent, 0)
+            run(k - 2, add_out_bias, 2)
+            run(k + 1, project_latent, 1)
+            run(k - 2, add_out_bias, 3)
+            run(k + 1, project_latent, 2)
+            run(k - 2, store_v)
 
-        iteration(-2)
-        iteration(-1)
+        for g in (2, 3):
+            load_x(g)
+        transpose_x(0, 0)
+        copy_x(0, 0)
+        repeat_biases()
+        quantise_x(0)
+        nc.vector.tensor_copy(out=gb_f32[:], in_=gb_rows[:])
+        project_rope(0)
+        for i in range(tiles_of(0)):
+            project_latent(0, i)
+        transpose_x(1, 0)
+        spread_gain_and_bias()
         iteration(0)
-        prepare_second_stage()
-        for k in range(1, len(groups) + 4):
+        regroup(nc, w2_grouped[:], w2_raw[:])
+        quantise(nc, w2_codes[:], w2_scales[:], w2_grouped[:])
+        for k in range(1, len(groups)):
             iteration(k)
+
+        last = len(groups) - 1
+        normalise(last, 0)
+        normalise(last, 1, nc.vector)
+        regroup_cn(last - 1)
+        for t in range(PACK):
+            transpose_z(last, t)
+            gain_and_bias(last, t)
+        quantise_cn(last - 1)
+        rotate(last - 2)
+        store_k(last - 2)
+        for i in range(tiles_of(last - 1)):
+            project_out(last - 1, i)
+            add_out_bias(last - 1, i)
+        store_v(last - 1)
+        rotate(last - 1)
+        store_k(last - 1)
+        regroup_cn(last)
+        quantise_cn(last)
+        for i in range(tiles_of(last)):
+            project_out(last, i)
+            add_out_bias(last, i)
+        store_v(last)
+        rotate(last, nc.vector)
+        store_k(last)

@@ -83,8 +83,7 @@ def tile_mla_pa_t_kernel(
         outs = ctx.enter_context(tc.tile_pool(name="outs", bufs=6))
         rot = ctx.enter_context(tc.tile_pool(name="rot", bufs=2))
         psum_s = ctx.enter_context(tc.psum_pool(name="psum_s", bufs=4))
-        psum_v = ctx.enter_context(tc.psum_pool(name="psum_v", bufs=3))
-        psum_r = ctx.enter_context(tc.psum_pool(name="psum_r", bufs=1))
+        psum_v = ctx.enter_context(tc.psum_pool(name="psum_v", bufs=4))
         ctx.enter_context(tc.manual_schedule())
 
         x_sb, x_t, x_grouped, x_codes, x_scales = {}, {}, {}, {}, {}
@@ -153,10 +152,14 @@ def tile_mla_pa_t_kernel(
         gb_f32 = consts.tile([P, P], F32)
         gb_col = consts.tile([P, 2 * PACK], F32)
 
-        def spread_gain_and_bias():
-            gb_t = psum_s.tile([P, TILES, P], F32, tag="to_scalar")
-            nc.tensor.transpose(gb_t[:, 0, :], gb_f32[:], ident[:])
-            nc.vector.tensor_copy(out=gb_col[:], in_=gb_t[:, 0, 0 : 2 * PACK])
+        def transpose_gain_and_bias():
+            nc.vector.tensor_copy(out=gb_f32[:], in_=gb_rows[:])
+            gb_bank = psum_v.tile([P, TILES, P], F32, tag="to_vector")
+            nc.tensor.transpose(gb_bank[:, 0, :], gb_f32[:], ident[:])
+            return gb_bank
+
+        def copy_gain_and_bias(gb_bank):
+            nc.vector.tensor_copy(out=gb_col[:], in_=gb_bank[:, 0, 0 : 2 * PACK])
 
         cos_pairs = consts.tile([P, SEQ_BLOCKS * TILES, ROT // 2, 2], BF16)
         neg_sin_sb = consts.tile([P, SEQ_BLOCKS, TILES, ROT // 2], BF16)
@@ -226,7 +229,7 @@ def tile_mla_pa_t_kernel(
             )
 
         def project_rope(g):
-            rope_bank = psum_r.tile([P, TILES, ROPE_COLS], F32)
+            rope_bank = psum_v.tile([P, TILES, ROPE_COLS], F32, tag="to_vector")
             k_rope[g] = rope_bank
             for i in range(tiles_of(g)):
                 project(g, i, rope_bank[:, i, :], slice(0, ROPE_COLS))
@@ -426,44 +429,44 @@ def tile_mla_pa_t_kernel(
 
         def iteration(k):
             run(k + 4, load_x)
-            run(k + 1, copy_x, 0)
-            run(k + 1, copy_x, 1)
+            run(k, add_rope_bias)
+            run(k, project_latent, 3)
+            run(k + 1, transpose_x, 0)
+            run(k + 1, transpose_x, 1)
             run(k - 1, normalise, 0)
             run(k - 1, normalise, 1)
             run(k - 1, normalise, 2)
             run(k - 1, normalise, 3)
-            run(k, add_rope_bias)
+            run(k + 1, copy_x, 0)
+            run(k + 1, copy_x, 1)
             run(k, add_bias_and_sum, 0)
-            run(k, project_latent, 3)
+            run(k - 2, regroup_cn)
             run(k, sum_squares, 0)
             run(k, add_bias_and_sum, 1)
-            run(k, sum_squares, 1)
             run(k - 3, rotate)
             run(k - 3, store_k)
             run(k - 1, transpose_z, 0)
             run(k - 1, transpose_z, 1)
             run(k - 1, transpose_z, 2)
             run(k - 1, transpose_z, 3)
-            run(k - 2, regroup_cn)
             run(k - 1, gain_and_bias, 0)
-            run(k + 2, transpose_x, 0)
+            run(k, sum_squares, 1)
             run(k, add_bias_and_sum, 2)
             run(k, sum_squares, 2)
             run(k - 2, quantise_cn)
             run(k - 1, gain_and_bias, 1)
             run(k - 2, project_out, 0)
             run(k - 2, project_out, 1)
+            run(k - 2, project_out, 2)
             run(k, add_bias_and_sum, 3)
             run(k, sum_squares, 3)
             run(k, inverse_deviation)
-            run(k - 2, project_out, 2)
+            run(k - 2, project_out, 3)
             run(k - 1, gain_and_bias, 2)
             run(k, shifts)
             run(k - 1, gain_and_bias, 3)
             run(k + 1, quantise_x)
             run(k - 2, add_out_bias, 0)
-            run(k - 2, project_out, 3)
-            run(k + 2, transpose_x, 1)
             run(k + 1, project_rope)
             run(k - 2, add_out_bias, 1)
             run(k + 1, project_latent, 0)
@@ -479,14 +482,13 @@ def tile_mla_pa_t_kernel(
         copy_x(0, 0)
         repeat_biases()
         quantise_x(0)
-        nc.vector.tensor_copy(out=gb_f32[:], in_=gb_rows[:])
         project_rope(0)
         for i in range(tiles_of(0)):
             project_latent(0, i)
-        transpose_x(1, 0)
-        spread_gain_and_bias()
+        gb_bank = transpose_gain_and_bias()
         iteration(0)
         regroup(nc, w2_grouped[:], w2_raw[:])
+        copy_gain_and_bias(gb_bank)
         quantise(nc, w2_codes[:], w2_scales[:], w2_grouped[:])
         for k in range(1, len(groups)):
             iteration(k)

from contextlib import ExitStack

import concourse.mybir as mybir
from concourse.masks import make_identity

F32 = mybir.dt.float32
BF16 = mybir.dt.bfloat16
U32 = mybir.dt.uint32
U8 = mybir.dt.uint8
FP8X4 = mybir.dt.float8_e4m3fn_x4
ALU = mybir.AluOpType
ACT = mybir.ActivationFunctionType

P = 128
PACK = 4
TOKENS = 4 * 2048
SEQ = 2048
DIM = 512
RANK = 512
ROPE_COLS = 128
KV_COLS = ROPE_COLS + RANK
NOPE_COLS = 256
V_COLS = 256
K_COLS = NOPE_COLS + ROPE_COLS
HEADS = 2
HEAD = K_COLS // HEADS
ROT = 64
TILES = 4
GROUP = TILES * P
BLOCKS = TOKENS // GROUP
SEQ_BLOCKS = SEQ // GROUP
EPS = 1e-5

FLOPS = 2 * TOKENS * (DIM * KV_COLS + RANK * (NOPE_COLS + V_COLS))


def regroup(nc, grouped, planes):
    nc.vector.tensor_copy(
        out=grouped.rearrange("p (c i) t -> p c t i", i=4),
        in_=planes.rearrange("p t (c i) -> p c t i", i=4),
    )


def quantise(nc, codes, scales, grouped):
    nc.vector.quantize_mx(
        out=codes.bitcast(FP8X4),
        scales=scales,
        in_=grouped.rearrange("p c t -> p (c t)"),
    )


def token_groups():
    groups = []
    for block in range(BLOCKS):
        tiles = TILES // 2 if block in (0, BLOCKS - 1) else TILES
        groups.extend((block, first, tiles) for first in range(0, TILES, tiles))
    return groups


def tile_mla_pa_t_kernel(
    tc, x, wkv_a_w, wkv_a_b, kvn_g, kvn_b, wk_w, wk_b, wv_w, wv_b, cos, sin, out_0, out_1
):
    nc = tc.nc
    x_rows = x.rearrange("b s d -> (b s) d")
    k_rows = out_0.rearrange("b s h e -> (b s) (h e)")
    v_rows = out_1.rearrange("b s h e -> (b s) (h e)")
    groups = token_groups()

    def rows_of(rows, g):
        block, first, n = groups[g]
        return rows[block * GROUP : (block + 1) * GROUP, :].rearrange("(p i) c -> p i c", i=TILES)[
            :, first : first + n, :
        ]

    def tiles_of(g):
        return groups[g][2]

    with ExitStack() as ctx:
        consts = ctx.enter_context(tc.tile_pool(name="consts", bufs=1))
        xin = ctx.enter_context(tc.tile_pool(name="xin", bufs=4))
        work = ctx.enter_context(tc.tile_pool(name="work", bufs=2))
        small = ctx.enter_context(tc.tile_pool(name="small", bufs=4))
        outs = ctx.enter_context(tc.tile_pool(name="outs", bufs=6))
        rot = ctx.enter_context(tc.tile_pool(name="rot", bufs=2))
        psum_s = ctx.enter_context(tc.psum_pool(name="psum_s", bufs=4))
        psum_v = ctx.enter_context(tc.psum_pool(name="psum_v", bufs=4))
        ctx.enter_context(tc.manual_schedule())

        x_sb, x_t, x_grouped, x_codes, x_scales = {}, {}, {}, {}, {}
        latent, k_rope, c, sums, sum_sq, neg_mean, rstd, shift, z, z_t = {}, {}, {}, {}, {}, {}, {}, {}, {}, {}
        cn_planes, cn_grouped, cn_codes, cn_scales, nope_v, kv_out = {}, {}, {}, {}, {}, {}

        def load_x(g):
            x_tile = xin.tile([P, TILES, DIM], BF16)
            nc.sync.dma_start(out=x_tile[:, 0 : tiles_of(g), :], in_=rows_of(x_rows, g))
            x_sb[g] = x_tile

        bias_rows = consts.tile([P, KV_COLS + NOPE_COLS + V_COLS], BF16)
        nc.vector.memset(bias_rows[:], 0.0)
        gb_rows = consts.tile([P, P], BF16)
        nc.vector.memset(gb_rows[:], 0.0)
        eps_col = consts.tile([P, 1], F32)
        nc.vector.memset(eps_col[:], EPS)
        ones = consts.tile([P, P], BF16)
        nc.vector.memset(ones[:], 1.0)
        ident = consts.tile([P, P], F32)
        make_identity(nc, ident[:])

        w1_raw = consts.tile([P, 2, 2, KV_COLS], BF16)
        w1_rows = wkv_a_w.rearrange("(u q e) c -> q u e c", u=2, e=2)
        w1_parts = (slice(0, KV_COLS // 2), slice(KV_COLS // 2, KV_COLS))
        for cols in w1_parts:
            for u in range(2):
                nc.sync.dma_start(out=w1_raw[:, u, :, cols], in_=w1_rows[:, u, :, cols])
        load_x(0)

        row = 0
        for bias in (wkv_a_b, wk_b, wv_b):
            n = bias.shape[0]
            nc.sync.dma_start(out=bias_rows[0:1, row : row + n], in_=bias.rearrange("(o n) -> o n", o=1))
            row += n
        nc.sync.dma_start(out=gb_rows[0:PACK, :], in_=kvn_g.rearrange("(t p) -> t p", p=P))
        nc.sync.dma_start(out=gb_rows[PACK : 2 * PACK, :], in_=kvn_b.rearrange("(t p) -> t p", p=P))
        warm = consts.tile([P, 1], F32)
        nc.scalar.activation(out=warm[:], in_=eps_col[:], func=ACT.Abs_reciprocal_sqrt)

        load_x(1)
        cos_sb = consts.tile([P, SEQ_BLOCKS, TILES, ROT // 2], BF16)
        nc.sync.dma_start(out=cos_sb[:], in_=cos.rearrange("(s p i) j -> p s i j", p=P, i=TILES))
        sin_sb = consts.tile([P, SEQ_BLOCKS, TILES, ROT // 2], BF16)
        nc.sync.dma_start(out=sin_sb[:], in_=sin.rearrange("(s p i) j -> p s i j", p=P, i=TILES))
        w2_raw = consts.tile([P, PACK, NOPE_COLS + V_COLS], BF16)
        nc.sync.dma_start(out=w2_raw[:, :, 0:NOPE_COLS], in_=wk_w.rearrange("(t p) n -> p t n", p=P))
        nc.sync.dma_start(out=w2_raw[:, :, NOPE_COLS:], in_=wv_w.rearrange("(t p) n -> p t n", p=P))

        b1_bc = consts.tile([P, KV_COLS], BF16)
        b2_bc = consts.tile([P, 2, NOPE_COLS], BF16)

        def repeat_biases():
            for out, first in (
                (b1_bc[:, 0:ROPE_COLS], 0),
                (b1_bc[:, ROPE_COLS:KV_COLS], ROPE_COLS),
                (b2_bc[:].rearrange("p s c -> p (s c)"), KV_COLS),
            ):
                n = out.shape[1]
                bias_bank = psum_v.tile([P, RANK], F32, tag="to_vector")
                nc.tensor.matmul(
                    out=bias_bank[:, 0:n], lhsT=ones[:], rhs=bias_rows[:, first : first + n], start=True, stop=True
                )
                nc.scalar.copy(out=out, in_=bias_bank[:, 0:n])

        gb_f32 = consts.tile([P, P], F32)
        gb_col = consts.tile([P, 2 * PACK], F32)

        def transpose_gain_and_bias():
            nc.vector.tensor_copy(out=gb_f32[:], in_=gb_rows[:])
            gb_bank = psum_v.tile([P, TILES, P], F32, tag="to_vector")
            nc.tensor.transpose(gb_bank[:, 0, :], gb_f32[:], ident[:])
            return gb_bank

        def copy_gain_and_bias(gb_bank):
            nc.vector.tensor_copy(out=gb_col[:], in_=gb_bank[:, 0, 0 : 2 * PACK])

        cos_pairs = consts.tile([P, SEQ_BLOCKS * TILES, ROT // 2, 2], BF16)
        neg_sin_sb = consts.tile([P, SEQ_BLOCKS, TILES, ROT // 2], BF16)
        for out, table, sign in (
            (cos_pairs[:, :, :, 0], cos_sb[:].rearrange("p s i j -> p (s i) j"), 1.0),
            (cos_pairs[:, :, :, 1], cos_sb[:].rearrange("p s i j -> p (s i) j"), 1.0),
            (neg_sin_sb[:], sin_sb[:], -1.0),
        ):
            nc.gpsimd.tensor_scalar(out=out, in0=table, scalar1=sign, scalar2=0.0, op0=ALU.mult, op1=ALU.add)

        w1_grouped = consts.tile([P, KV_COLS, PACK], BF16, align_bytes=64)
        w1_codes = consts.tile([P, KV_COLS], U32, align_bytes=64)
        w1_scales = consts.tile([P, KV_COLS], U8, align_bytes=64)
        for cols in w1_parts:
            regroup(nc, w1_grouped[:, cols, :], w1_raw[:, :, :, cols].rearrange("p u e c -> p (u e) c"))
        for cols in (slice(0, ROPE_COLS), slice(ROPE_COLS, KV_COLS)):
            quantise(nc, w1_codes[:, cols], w1_scales[:, cols], w1_grouped[:, cols, :])

        w2_grouped = consts.tile([P, NOPE_COLS + V_COLS, PACK], BF16, align_bytes=64)
        w2_codes = consts.tile([P, NOPE_COLS + V_COLS], U32, align_bytes=64)
        w2_scales = consts.tile([P, NOPE_COLS + V_COLS], U8, align_bytes=64)

        def transpose_x(g, half):
            if 2 * half >= tiles_of(g):
                return
            x_bank = psum_s.tile([P, 2, 2, P], F32, tag="to_scalar")
            x_t[g, half] = x_bank
            for i in range(2):
                x_words = x_sb[g][:, 2 * half + i, :].bitcast(F32)
                for u in range(2):
                    nc.tensor.transpose(x_bank[:, i, u, :], x_words[:, u * P : (u + 1) * P], ident[:])

        def copy_x(g, half):
            if 2 * half >= tiles_of(g):
                return
            if half == 0:
                grouped_tile = work.tile([P, GROUP * PACK], BF16, align_bytes=64)
                x_grouped[g] = grouped_tile
            nc.scalar.copy(
                out=x_grouped[g][:]
                .bitcast(F32)[:, half * GROUP : (half + 1) * GROUP]
                .rearrange("p (i w u) -> p i w u", i=2, u=2),
                in_=x_t[g, half][:].rearrange("p i u w -> p i w u"),
            )

        def quantise_x(g):
            codes_tile = work.tile([P, GROUP], U32, align_bytes=64)
            scales_tile = work.tile([P, GROUP], U8, align_bytes=64)
            x_codes[g], x_scales[g] = codes_tile, scales_tile
            cols = slice(0, tiles_of(g) * P)
            nc.vector.quantize_mx(
                out=codes_tile[:, cols].bitcast(FP8X4),
                scales=scales_tile[:, cols],
                in_=x_grouped[g][:, 0 : tiles_of(g) * P * PACK],
            )

        def project(g, i, out, cols):
            tokens = slice(i * P, (i + 1) * P)
            nc.tensor.matmul_mx(
                out=out,
                lhsT=x_codes[g][:, tokens].bitcast(FP8X4),
                lhsT_scale=x_scales[g][:, tokens],
                rhs=w1_codes[:, cols].bitcast(FP8X4),
                rhs_scale=w1_scales[:, cols],
                start=True,
                stop=True,
            )

        def project_rope(g):
            rope_bank = psum_v.tile([P, TILES, ROPE_COLS], F32, tag="to_vector")
            k_rope[g] = rope_bank
            for i in range(tiles_of(g)):
                project(g, i, rope_bank[:, i, :], slice(0, ROPE_COLS))

        def project_latent(g, i):
            if i < tiles_of(g):
                latent_bank = psum_v.tile([P, RANK], F32, tag="to_vector")
                latent[g, i] = latent_bank
                project(g, i, latent_bank[:], slice(ROPE_COLS, KV_COLS))

        def add_bias_and_sum(g, i):
            if i >= tiles_of(g):
                return
            if i == 0:
                c_tile = work.tile([P, TILES, RANK], F32)
                sums_tile = small.tile([P, TILES], F32)
                c[g], sums[g] = c_tile, sums_tile
            nc.vector.scalar_tensor_tensor(
                out=c[g][:, i, :],
                in0=latent[g, i][:],
                scalar=1.0,
                in1=b1_bc[:, ROPE_COLS:KV_COLS],
                op0=ALU.mult,
                op1=ALU.add,
                accum_out=sums[g][:, i : i + 1],
            )

        def sum_squares(g, i):
            if i >= tiles_of(g):
                return
            if i == 0:
                sum_sq_tile = small.tile([P, TILES], F32)
                sum_sq[g] = sum_sq_tile
            squares = work.tile([P, RANK], BF16)
            nc.scalar.activation(
                out=squares[:],
                in_=c[g][:, i, :],
                func=ACT.Square,
                bias=sums[g][:, i : i + 1],
                scale=-1.0 * RANK,
                accum_out=sum_sq[g][:, i : i + 1],
            )

        def inverse_deviation(g):
            n = tiles_of(g)
            neg_mean_tile = small.tile([P, TILES], F32)
            rstd_tile = small.tile([P, TILES], F32)
            neg_mean[g], rstd[g] = neg_mean_tile, rstd_tile
            nc.scalar.mul(neg_mean_tile[:, 0:n], sums[g][:, 0:n], -1.0 / RANK)
            nc.scalar.activation(
                out=rstd_tile[:, 0:n],
                in_=sum_sq[g][:, 0:n],
                func=ACT.Abs_reciprocal_sqrt,
                bias=eps_col[:],
                scale=1.0 / RANK**3,
            )

        def shifts(g):
            shift_tile = small.tile([P, TILES], F32)
            shift[g] = shift_tile
            for i in range(tiles_of(g)):
                nc.scalar.activation(
                    out=shift_tile[:, i : i + 1],
                    in_=neg_mean[g][:, i : i + 1],
                    func=ACT.Copy,
                    scale=rstd[g][:, i : i + 1],
                )

        def add_rope_bias(g):
            kv_tile = outs.tile([P, 2, TILES, K_COLS], F32)
            kv_out[g] = kv_tile
            n = tiles_of(g)
            nc.vector.tensor_tensor(
                out=kv_tile[:, 0, 0:n, NOPE_COLS:K_COLS],
                in0=k_rope[g][:, 0:n, :],
                in1=b1_bc[:, 0:ROPE_COLS].unsqueeze(1).to_broadcast([P, n, ROPE_COLS]),
                op=ALU.add,
            )

        def normalise(g, i, engine=None):
            if i >= tiles_of(g):
                return
            if i == 0:
                z_tile = work.tile([P, TILES, RANK], F32)
                z[g] = z_tile
            if engine is None and i >= TILES // 2:
                engine = nc.gpsimd
            if engine is None:
                nc.scalar.activation(
                    out=z[g][:, i, :],
                    in_=c[g][:, i, :],
                    func=ACT.Identity,
                    bias=shift[g][:, i : i + 1],
                    scale=rstd[g][:, i : i + 1],
                )
            else:
                engine.tensor_scalar(
                    out=z[g][:, i, :],
                    in0=c[g][:, i, :],
                    scalar1=rstd[g][:, i : i + 1],
                    scalar2=shift[g][:, i : i + 1],
                    op0=ALU.mult,
                    op1=ALU.add,
                )

        def transpose_z(g, t):
            z_bank = psum_s.tile([P, TILES, P], F32, tag="to_scalar")
            z_t[g, t] = z_bank
            for i in range(tiles_of(g)):
                nc.tensor.transpose(z_bank[:, i, :], z[g][:, i, t * P : (t + 1) * P], ident[:])

        def gain_and_bias(g, t):
            if t == 0:
                planes_tile = work.tile([P, PACK, GROUP], BF16)
                cn_planes[g] = planes_tile
            n = tiles_of(g)
            nc.scalar.activation(
                out=cn_planes[g][:, t, 0 : n * P],
                in_=z_t[g, t][:, 0:n, :].rearrange("p i w -> p (i w)"),
                func=ACT.Identity,
                bias=gb_col[:, PACK + t : PACK + t + 1],
                scale=gb_col[:, t : t + 1],
            )

        def regroup_cn(g):
            cn_grouped_tile = work.tile([P, GROUP, PACK], BF16, align_bytes=64)
            cn_grouped[g] = cn_grouped_tile
            cols = slice(0, tiles_of(g) * P)
            regroup(nc, cn_grouped_tile[:, cols, :], cn_planes[g][:, :, cols])

        def quantise_cn(g):
            cn_codes_tile = work.tile([P, GROUP], U32, align_bytes=64)
            cn_scales_tile = work.tile([P, GROUP], U8, align_bytes=64)
            cn_codes[g], cn_scales[g] = cn_codes_tile, cn_scales_tile
            cols = slice(0, tiles_of(g) * P)
            quantise(nc, cn_codes_tile[:, cols], cn_scales_tile[:, cols], cn_grouped[g][:, cols, :])

        def project_out(g, i):
            if i >= tiles_of(g):
                return
            tokens = slice(i * P, (i + 1) * P)
            out_bank = psum_v.tile([P, 2, NOPE_COLS], F32, tag="to_vector")
            nope_v[g, i] = out_bank
            nc.tensor.matmul_mx(
                out=out_bank[:].rearrange("p s c -> p (s c)"),
                lhsT=cn_codes[g][:, tokens].bitcast(FP8X4),
                lhsT_scale=cn_scales[g][:, tokens],
                rhs=w2_codes[:].bitcast(FP8X4),
                rhs_scale=w2_scales[:],
                start=True,
                stop=True,
            )

        def add_out_bias(g, i):
            if i < tiles_of(g):
                nc.vector.tensor_tensor(
                    out=kv_out[g][:, :, i, 0:NOPE_COLS], in0=nope_v[g, i][:], in1=b2_bc[:], op=ALU.add
                )

        def rotate(g, engine=nc.gpsimd):
            block, first, n = groups[g]
            s = block % SEQ_BLOCKS
            positions = slice(first, first + n)
            cos_g = cos_pairs[:, s * TILES + first : s * TILES + first + n, :, :].rearrange("p i j e -> p i (j e)")
            rotated = kv_out[g][:, 0, 0:n, :].rearrange("p i (h e) -> p i h e", h=HEADS)[:, :, :, HEAD - ROT : HEAD]
            pairs = rotated.rearrange("p i h (j e) -> p i h j e", e=2)
            by_cos = rot.tile([P, n, HEADS, ROT], F32, tag="by_cos")
            by_sin = rot.tile([P, 2, n, HEADS, ROT // 2], F32, tag="by_sin")
            engine.tensor_tensor(
                out=by_cos[:], in0=rotated, in1=cos_g.unsqueeze(2).to_broadcast([P, n, HEADS, ROT]), op=ALU.mult
            )
            for e, table in ((0, neg_sin_sb), (1, sin_sb)):
                engine.tensor_tensor(
                    out=by_sin[:, e],
                    in0=pairs[:, :, :, :, 1 - e],
                    in1=table[:, s, positions, :].unsqueeze(2).to_broadcast([P, n, HEADS, ROT // 2]),
                    op=ALU.mult,
                )
            engine.tensor_tensor(
                out=pairs,
                in0=by_cos[:].rearrange("p i h (j e) -> p i h j e", e=2),
                in1=by_sin[:].rearrange("p e i h j -> p i h j e"),
                op=ALU.add,
            )

        def store_k(g):
            n = tiles_of(g)
            nc.sync.dma_start(out=rows_of(k_rows, g), in_=kv_out[g][:, 0, 0:n, :])

        def store_v(g):
            n = tiles_of(g)
            nc.sync.dma_start(out=rows_of(v_rows, g), in_=kv_out[g][:, 1, 0:n, 0:V_COLS])

        def run(g, step, *args):
            if 0 <= g < len(groups):
                step(g, *args)

        def iteration(k):
            run(k + 4, load_x)
            run(k, add_rope_bias)
            run(k, project_latent, 3)
            run(k + 1, transpose_x, 0)
            run(k + 1, transpose_x, 1)
            run(k - 1, normalise, 0)
            run(k - 1, normalise, 1)
            run(k - 1, normalise, 2)
            run(k - 1, normalise, 3)
            run(k + 1, copy_x, 0)
            run(k + 1, copy_x, 1)
            run(k, add_bias_and_sum, 0)
            run(k - 2, regroup_cn)
            run(k, sum_squares, 0)
            run(k, add_bias_and_sum, 1)
            run(k - 3, rotate)
            run(k - 3, store_k)
            run(k - 1, transpose_z, 0)
            run(k - 1, transpose_z, 1)
            run(k - 1, transpose_z, 2)
            run(k - 1, transpose_z, 3)
            run(k - 1, gain_and_bias, 0)
            run(k, sum_squares, 1)
            run(k, add_bias_and_sum, 2)
            run(k, sum_squares, 2)
            run(k - 2, quantise_cn)
            run(k - 1, gain_and_bias, 1)
            run(k - 2, project_out, 0)
            run(k - 2, project_out, 1)
            run(k - 2, project_out, 2)
            run(k, add_bias_and_sum, 3)
            run(k, sum_squares, 3)
            run(k, inverse_deviation)
            run(k - 2, project_out, 3)
            run(k - 1, gain_and_bias, 2)
            run(k, shifts)
            run(k - 1, gain_and_bias, 3)
            run(k + 1, quantise_x)
            run(k - 2, add_out_bias, 0)
            run(k + 1, project_rope)
            run(k - 2, add_out_bias, 1)
            run(k + 1, project_latent, 0)
            run(k - 2, add_out_bias, 2)
            run(k + 1, project_latent, 1)
            run(k - 2, add_out_bias, 3)
            run(k + 1, project_latent, 2)
            run(k - 2, store_v)

        for g in (2, 3):
            load_x(g)
        transpose_x(0, 0)
        copy_x(0, 0)
        repeat_biases()
        quantise_x(0)
        project_rope(0)
        for i in range(tiles_of(0)):
            project_latent(0, i)
        gb_bank = transpose_gain_and_bias()
        iteration(0)
        regroup(nc, w2_grouped[:], w2_raw[:])
        copy_gain_and_bias(gb_bank)
        quantise(nc, w2_codes[:], w2_scales[:], w2_grouped[:])
        for k in range(1, len(groups)):
            iteration(k)

        last = len(groups) - 1
        normalise(last, 0)
        normalise(last, 1, nc.vector)
        regroup_cn(last - 1)
        for t in range(PACK):
            transpose_z(last, t)
            gain_and_bias(last, t)
        quantise_cn(last - 1)
        rotate(last - 2)
        store_k(last - 2)
        for i in range(tiles_of(last - 1)):
            project_out(last - 1, i)
            add_out_bias(last - 1, i)
        store_v(last - 1)
        rotate(last - 1)
        store_k(last - 1)
        regroup_cn(last)
        quantise_cn(last)
        for i in range(tiles_of(last)):
            project_out(last, i)
            add_out_bias(last, i)
        store_v(last)
        rotate(last, nc.vector)
        store_k(last)
